import numpy as np
import ml_dtypes


def mxq(x, axis, fmt="e4m3"):
    dtype, down = {"e4m3": (ml_dtypes.float8_e4m3fn, 7), "e5m2": (ml_dtypes.float8_e5m2, 14)}[fmt]
    v = np.moveaxis(np.asarray(x, np.float32).astype(ml_dtypes.bfloat16).astype(np.float64), axis, -1)
    blocks = v.reshape(v.shape[:-1] + (-1, 32))
    amax = np.abs(blocks).max(-1, keepdims=True)
    byte = np.maximum(np.where(amax > 0, np.frexp(amax)[1] - 1 + 127, 0) - down, 1)
    scale = np.exp2(byte - 127.0)
    codes = (blocks / scale).astype(np.float32).astype(dtype).astype(np.float64)
    return np.moveaxis((codes * scale).reshape(v.shape), -1, axis)


WIDE = False


def mx_kscale(k):
    if not WIDE:
        return np.ones(k)
    levels = np.array([10, -10, 5, -5, 0])
    a = np.random.permutation(np.resize(levels, k // 512 * 4)).reshape(k // 512, 4)
    idx = np.arange(k)
    return np.exp2(a[idx // 512, idx % 128 // 32])


BF16 = ml_dtypes.bfloat16


def bf(x):
    return np.asarray(x, np.float32).astype(BF16)


def f64(x):
    return np.asarray(x).astype(np.float64)


B, S, D, R, V = 128, 16, 1024, 512, 8192


def erf(z):
    a = np.minimum(np.abs(z), 6.0)
    a2 = 2.0 * a * a
    term = a.copy()
    tot = a.copy()
    for n in range(1, 120):
        term = term * a2 / (2.0 * n + 1.0)
        tot = tot + term
    return np.sign(z) * (2.0 / np.sqrt(np.pi)) * np.exp(-a * a) * tot


def gelu_erf(v):
    return 0.5 * v * (1.0 + erf(v / np.sqrt(2.0)))


def setup_inputs():
    s, u = mx_kscale(D), mx_kscale(D)
    su = np.concatenate([s, u])
    return {
        "x": bf(np.random.standard_normal((B, S, D)) * s),
        "wk": bf(np.random.standard_normal((B, D)) * 0.4 * u),
        "i_w1": bf(np.random.standard_normal((D + D, D)) / np.sqrt(D) / su[:, None]),
        "i_b1": bf(np.random.standard_normal(D) * 0.2),
        "i_w2": bf(np.random.standard_normal((D, D)) * 1.4 / np.sqrt(D)),
        "i_b2": bf(np.random.standard_normal(D) * 0.2),
    }


def reference(x, wk, i_w1, i_b1, i_w2, i_b2):
    w1 = f64(i_w1)
    tok = mxq(f64(x), 2, "e4m3") @ mxq(w1[:D], 0, "e4m3")
    ctx = mxq(f64(wk), 1, "e4m3") @ mxq(w1[D:], 0, "e4m3")
    g = gelu_erf(tok + ctx[:, None, :] + f64(i_b1))
    return np.tanh((mxq(g, 2, "e4m3") @ mxq(f64(i_w2), 0, "e4m3")) + f64(i_b2))

@@ -1,0 +1,281 @@
+from contextlib import ExitStack
+
+import concourse.mybir as mybir
+from concourse.masks import make_identity
+
+F32 = mybir.dt.float32
+BF16 = mybir.dt.bfloat16
+U32 = mybir.dt.uint32
+U8 = mybir.dt.uint8
+FP8X4 = mybir.dt.float8_e4m3fn_x4
+ADD = mybir.AluOpType.add
+GELU = mybir.ActivationFunctionType.Gelu
+TANH = mybir.ActivationFunctionType.Tanh
+
+P = 128
+PACK = 4
+K_PASS = P * PACK
+B, S, D = 128, 16, 1024
+PASSES = D // K_PASS
+BANK = 512
+HALVES = D // BANK
+PAIR = 2
+GROUPS = S // PAIR
+RUN = 4
+VECTOR_COLS = 512
+FIRST_W2_GROUP = 2
+
+FLOPS = 2 * (B * S * D * D * 2 + B * D * D)
+
+
+def tile_universalknowledgeintegrator_pb_kernel(tc, x, wk, i_w1, i_b1, i_w2, i_b2, out):
+    nc = tc.nc
+    with ExitStack() as ctx:
+        ctx.enter_context(tc.manual_schedule())
+        keep = ctx.enter_context(tc.tile_pool(name="keep", bufs=1))
+        x_in = ctx.enter_context(tc.tile_pool(name="x_in", bufs=GROUPS))
+        w_in = ctx.enter_context(tc.tile_pool(name="w_in", bufs=3 * PASSES))
+        w_stage = ctx.enter_context(tc.tile_pool(name="w_stage", bufs=3))
+        x_stage = ctx.enter_context(tc.tile_pool(name="x_stage", bufs=2))
+        x_mx = ctx.enter_context(tc.tile_pool(name="x_mx", bufs=3))
+        g_stage = ctx.enter_context(tc.tile_pool(name="g_stage", bufs=3))
+        o_stage = ctx.enter_context(tc.tile_pool(name="o_stage", bufs=4))
+        psum_t = ctx.enter_context(tc.psum_pool(name="psum_t", bufs=PAIR))
+        psum_mm = ctx.enter_context(tc.psum_pool(name="psum_mm", bufs=8 - PAIR))
+
+        warm = keep.tile([P, 1], F32)
+        nc.vector.memset(warm[:], 0.0)
+        nc.scalar.activation(out=warm[:], in_=warm[:], func=GELU)
+        ident_f32 = keep.tile([P, P], F32)
+        make_identity(nc, ident_f32[:])
+        ident_bf16 = keep.tile([P, P], BF16)
+        make_identity(nc, ident_bf16[:])
+        b1_rows = keep.tile([P, P], BF16)
+        nc.vector.memset(b1_rows[:], 0.0)
+
+        def load_w1_pass(c):
+            raw = w_in.tile([P, PACK, D], BF16, tag="w_raw")
+            nc.sync.dma_start(
+                out=raw[:].rearrange("p (u e) n -> p u (e n)", u=2),
+                in_=i_w1[c * K_PASS : (c + 1) * K_PASS, :].rearrange("(u p e) n -> p u (e n)", u=2, e=2),
+            )
+            return raw
+
+        def load_w2_pass(c):
+            raw = w_in.tile([P, PACK, D], BF16, tag="w_raw")
+            nc.sync.dma_start(
+                out=raw[:], in_=i_w2[c * K_PASS : (c + 1) * K_PASS, :].rearrange("(t p) n -> p t n", p=P)
+            )
+            return raw
+
+        def load_x_pair(j):
+            raw = x_in.tile([P, PAIR, D], BF16, tag="x_raw")
+            nc.sync.dma_start(out=raw[:], in_=x[:, j * PAIR : (j + 1) * PAIR, :])
+            return raw
+
+        wk_raw = keep.tile([P, D], BF16)
+        nc.sync.dma_start(out=wk_raw[:], in_=wk)
+        nc.sync.dma_start(out=b1_rows[0 : D // P, :], in_=i_b1.rearrange("(r c) -> r c", c=P))
+        w1_raw = {}
+        x_raw = {}
+        w2_raw = {}
+        w1_raw[2] = load_w1_pass(2)
+        w1_raw[3] = load_w1_pass(3)
+        x_raw[0] = load_x_pair(0)
+        w1_raw[0] = load_w1_pass(0)
+        w1_raw[1] = load_w1_pass(1)
+        x_raw[1] = load_x_pair(1)
+        for c in range(PASSES):
+            w2_raw[c] = load_w2_pass(c)
+        for j in range(2, GROUPS):
+            x_raw[j] = load_x_pair(j)
+        b2_all = keep.tile([P, D], BF16)
+        nc.sync.dma_start(out=b2_all[:], in_=i_b2.partition_broadcast(P))
+
+        w1_codes = keep.tile([P, 2 * PASSES, D], U32, align_bytes=64)
+        w1_scales = keep.tile([P, 2 * PASSES, D], U8, align_bytes=64)
+        w2_codes = keep.tile([P, PASSES, D], U32, align_bytes=64)
+        w2_scales = keep.tile([P, PASSES, D], U8, align_bytes=64)
+        wk_codes = keep.tile([P, PASSES * B], U32, align_bytes=64)
+        wk_scales = keep.tile([P, PASSES * B], U8, align_bytes=64)
+        g_codes = keep.tile([P, S, PASSES, B], U32, align_bytes=64)
+        g_scales = keep.tile([P, S, PASSES, B], U8, align_bytes=64)
+
+        def regroup_weight(raw):
+            grouped = w_stage.tile([P, D, PACK], BF16, tag="w_grouped", align_bytes=64)
+            for copy, cols in (
+                (nc.vector.tensor_copy, slice(0, VECTOR_COLS)),
+                (nc.scalar.copy, slice(VECTOR_COLS, D)),
+            ):
+                copy(
+                    out=grouped[:, cols, :].rearrange("p (c i) t -> p c t i", i=RUN),
+                    in_=raw[:, :, cols].rearrange("p t (c i) -> p c t i", i=RUN),
+                )
+            return grouped
+
+        def quantise_weight(grouped, codes, scales, half):
+            cols = slice(half * BANK, (half + 1) * BANK)
+            nc.vector.quantize_mx(
+                out=codes[:, cols].bitcast(FP8X4),
+                scales=scales[:, cols],
+                in_=grouped[:, cols, :].rearrange("p n t -> p (n t)"),
+            )
+
+        def transpose_tile(rows):
+            words = rows.bitcast(F32)
+            turned = psum_t.tile([P, PASSES * 2, B], F32, tag="turned")
+            for q in range(PASSES * 2):
+                nc.tensor.transpose(turned[:, q, :], words[:, q * P : (q + 1) * P], ident_f32[:])
+            return turned
+
+        def regroup_tile(turned, grouped_words):
+            nc.scalar.copy(
+                out=grouped_words.rearrange("p (c b u) -> p c b u", c=PASSES, u=2),
+                in_=turned[:].rearrange("p (c u) b -> p c b u", u=2),
+            )
+
+        def prepare_x_pair(j):
+            grouped = x_stage.tile([P, PAIR * D], BF16, tag="x_grouped", align_bytes=64)
+            turned = [transpose_tile(x_raw[j][:, i, :]) for i in range(PAIR)]
+            for i in range(PAIR):
+                regroup_tile(turned[i], grouped[:, i * D : (i + 1) * D].bitcast(F32))
+            return grouped
+
+        def quantise_x_pair(grouped):
+            codes = x_mx.tile([P, PAIR, PASSES, B], U32, tag="x_codes", align_bytes=64)
+            scales = x_mx.tile([P, PAIR, PASSES, B], U8, tag="x_scales", align_bytes=64)
+            nc.vector.quantize_mx(
+                out=codes[:].rearrange("p i c b -> p (i c b)").bitcast(FP8X4),
+                scales=scales[:].rearrange("p i c b -> p (i c b)"),
+                in_=grouped[:],
+            )
+            return codes, scales
+
+        def first_layer_bank(first_pass, half, codes, scales):
+            bank = psum_mm.tile([P, PACK, B], F32, tag="bank")
+            for t in range(PACK):
+                cols = slice(half * BANK + t * P, half * BANK + (t + 1) * P)
+                for c in range(PASSES):
+                    nc.tensor.matmul_mx(
+                        out=bank[:, t, :],
+                        lhsT=w1_codes[:, first_pass + c, cols].bitcast(FP8X4),
+                        lhsT_scale=w1_scales[:, first_pass + c, cols],
+                        rhs=codes[c].bitcast(FP8X4),
+                        rhs_scale=scales[c],
+                        start=(c == 0),
+                        stop=(c == PASSES - 1),
+                    )
+            return bank
+
+        wk_turned = transpose_tile(wk_raw[:])
+        wk_grouped = keep.tile([P, D], BF16, align_bytes=64)
+        regroup_tile(wk_turned, wk_grouped[:].bitcast(F32))
+        b1_turned = psum_t.tile([P, P], BF16, tag="turned")
+        nc.tensor.transpose(b1_turned[:], b1_rows[:], ident_bf16[:])
+
+        grouped_2 = regroup_weight(w1_raw[2])
+        nc.vector.quantize_mx(out=wk_codes[:].bitcast(FP8X4), scales=wk_scales[:], in_=wk_grouped[:])
+        b1_cols = keep.tile([P, D // P], F32)
+        nc.vector.tensor_copy(out=b1_cols[:], in_=b1_turned[:, 0 : D // P])
+        quantise_weight(grouped_2, w1_codes[:, 2, :], w1_scales[:, 2, :], 0)
+        grouped_3 = regroup_weight(w1_raw[3])
+        quantise_weight(grouped_2, w1_codes[:, 2, :], w1_scales[:, 2, :], 1)
+        quantise_weight(grouped_3, w1_codes[:, 3, :], w1_scales[:, 3, :], 0)
+        x_grouped = {0: prepare_x_pair(0)}
+        quantise_weight(grouped_3, w1_codes[:, 3, :], w1_scales[:, 3, :], 1)
+
+        wk_c = [wk_codes[:, c * B : (c + 1) * B] for c in range(PASSES)]
+        wk_s = [wk_scales[:, c * B : (c + 1) * B] for c in range(PASSES)]
+        know_banks = [first_layer_bank(PASSES, half, wk_c, wk_s) for half in range(HALVES)]
+
+        grouped_0 = regroup_weight(w1_raw[0])
+        x_quant = {0: quantise_x_pair(x_grouped[0])}
+        quantise_weight(grouped_0, w1_codes[:, 0, :], w1_scales[:, 0, :], 0)
+        grouped_1 = regroup_weight(w1_raw[1])
+        know = keep.tile([P, HALVES, B, PACK], F32)
+        for half in range(HALVES):
+            nc.vector.tensor_tensor(
+                out=know[:, half],
+                in0=know_banks[half][:].rearrange("p t b -> p b t"),
+                in1=b1_cols[:, half * PACK : (half + 1) * PACK].unsqueeze(1).to_broadcast([P, B, PACK]),
+                op=ADD,
+            )
+        quantise_weight(grouped_0, w1_codes[:, 0, :], w1_scales[:, 0, :], 1)
+        quantise_weight(grouped_1, w1_codes[:, 1, :], w1_scales[:, 1, :], 0)
+        x_grouped[1] = prepare_x_pair(1)
+        quantise_weight(grouped_1, w1_codes[:, 1, :], w1_scales[:, 1, :], 1)
+
+        def multiply_tile(j, i):
+            codes, scales = x_quant[j]
+            tile_c = [codes[:, i, c, :] for c in range(PASSES)]
+            tile_s = [scales[:, i, c, :] for c in range(PASSES)]
+            return [first_layer_bank(0, half, tile_c, tile_s) for half in range(HALVES)]
+
+        def add_knowledge(banks):
+            pre = g_stage.tile([P, HALVES, B, PACK], F32, tag="pre")
+            for half in range(HALVES):
+                nc.vector.tensor_tensor(
+                    out=pre[:, half], in0=banks[half][:].rearrange("p t b -> p b t"), in1=know[:, half], op=ADD
+                )
+            return pre
+
+        def gelu_tile(pre, g_grouped, i):
+            nc.scalar.activation(
+                out=g_grouped[:, i * D : (i + 1) * D], in_=pre[:].rearrange("p c b t -> p (c b t)"), func=GELU
+            )
+
+        def quantise_g_pair(j, g_grouped):
+            tiles = slice(j * PAIR, (j + 1) * PAIR)
+            nc.vector.quantize_mx(
+                out=g_codes[:, tiles].rearrange("p s c b -> p (s c b)").bitcast(FP8X4),
+                scales=g_scales[:, tiles].rearrange("p s c b -> p (s c b)"),
+                in_=g_grouped[:],
+            )
+
+        g_grouped = {}
+        w2_grouped = {}
+        for j in range(GROUPS):
+            w2_pass = j - FIRST_W2_GROUP
+            if 0 <= w2_pass < PASSES:
+                w2_grouped[w2_pass] = regroup_weight(w2_raw[w2_pass])
+            g_grouped[j] = g_stage.tile([P, PAIR * D], BF16, tag="g_grouped", bufs=2, align_bytes=64, name="g_grouped")
+
+            banks = multiply_tile(j, 0)
+            pre = add_knowledge(banks)
+            if j + 1 < GROUPS:
+                x_quant[j + 1] = quantise_x_pair(x_grouped[j + 1])
+            gelu_tile(pre, g_grouped[j], 0)
+            if j + 2 < GROUPS:
+                x_grouped[j + 2] = prepare_x_pair(j + 2)
+            banks = multiply_tile(j, 1)
+            pre = add_knowledge(banks)
+            gelu_tile(pre, g_grouped[j], 1)
+            if j >= 1:
+                quantise_g_pair(j - 1, g_grouped[j - 1])
+            if 0 <= w2_pass < PASSES:
+                for half in range(HALVES):
+                    quantise_weight(w2_grouped[w2_pass], w2_codes[:, w2_pass, :], w2_scales[:, w2_pass, :], half)
+
+        def finish_tile(s):
+            z = o_stage.tile([P, D], F32, tag="z")
+            for half in range(HALVES):
+                cols = slice(half * BANK, (half + 1) * BANK)
+                bank = psum_mm.tile([P, BANK], F32, tag="bank")
+                for c in range(PASSES):
+                    nc.tensor.matmul_mx(
+                        out=bank[:],
+                        lhsT=g_codes[:, s, c, :].bitcast(FP8X4),
+                        lhsT_scale=g_scales[:, s, c, :],
+                        rhs=w2_codes[:, c, cols].bitcast(FP8X4),
+                        rhs_scale=w2_scales[:, c, cols],
+                        start=(c == 0),
+                        stop=(c == PASSES - 1),
+                    )
+                nc.vector.tensor_tensor(out=z[:, cols], in0=bank[:], in1=b2_all[:, cols], op=ADD)
+            nc.scalar.activation(out=z[:], in_=z[:], func=TANH)
+            nc.sync.dma_start(out=out[:, s, :], in_=z[:])
+
+        finish_tile(0)
+        quantise_g_pair(GROUPS - 1, g_grouped[GROUPS - 1])
+        for s in range(1, S):
+            finish_tile(s)

@@ -19,11 +19,12 @@ B, S, D = 128, 16, 1024
 PASSES = D // K_PASS
 BANK = 512
 HALVES = D // BANK
+PSUM_BANKS = 8
 PAIR = 2
 GROUPS = S // PAIR
+LAG = 2
 RUN = 4
 VECTOR_COLS = 512
-FIRST_W2_GROUP = 2
 
 FLOPS = 2 * (B * S * D * D * 2 + B * D * D)
 
@@ -39,9 +40,9 @@ def tile_universalknowledgeintegrator_pb_kernel(tc, x, wk, i_w1, i_b1, i_w2, i_b
         x_stage = ctx.enter_context(tc.tile_pool(name="x_stage", bufs=2))
         x_mx = ctx.enter_context(tc.tile_pool(name="x_mx", bufs=3))
         g_stage = ctx.enter_context(tc.tile_pool(name="g_stage", bufs=3))
-        o_stage = ctx.enter_context(tc.tile_pool(name="o_stage", bufs=4))
+        o_stage = ctx.enter_context(tc.tile_pool(name="o_stage", bufs=5))
         psum_t = ctx.enter_context(tc.psum_pool(name="psum_t", bufs=PAIR))
-        psum_mm = ctx.enter_context(tc.psum_pool(name="psum_mm", bufs=8 - PAIR))
+        psum_mm = ctx.enter_context(tc.psum_pool(name="psum_mm", bufs=PSUM_BANKS - PAIR))
 
         warm = keep.tile([P, 1], F32)
         nc.vector.memset(warm[:], 0.0)
@@ -73,13 +74,13 @@ def tile_universalknowledgeintegrator_pb_kernel(tc, x, wk, i_w1, i_b1, i_w2, i_b
             nc.sync.dma_start(out=raw[:], in_=x[:, j * PAIR : (j + 1) * PAIR, :])
             return raw
 
-        wk_raw = keep.tile([P, D], BF16)
-        nc.sync.dma_start(out=wk_raw[:], in_=wk)
-        nc.sync.dma_start(out=b1_rows[0 : D // P, :], in_=i_b1.rearrange("(r c) -> r c", c=P))
         w1_raw = {}
         x_raw = {}
         w2_raw = {}
         w1_raw[2] = load_w1_pass(2)
+        wk_raw = keep.tile([P, D], BF16)
+        nc.sync.dma_start(out=wk_raw[:], in_=wk)
+        nc.sync.dma_start(out=b1_rows[0 : D // P, :], in_=i_b1.rearrange("(r c) -> r c", c=P))
         w1_raw[3] = load_w1_pass(3)
         x_raw[0] = load_x_pair(0)
         w1_raw[0] = load_w1_pass(0)
@@ -87,7 +88,8 @@ def tile_universalknowledgeintegrator_pb_kernel(tc, x, wk, i_w1, i_b1, i_w2, i_b
         x_raw[1] = load_x_pair(1)
         for c in range(PASSES):
             w2_raw[c] = load_w2_pass(c)
-        for j in range(2, GROUPS):
+            x_raw[2 + c] = load_x_pair(2 + c)
+        for j in range(2 + PASSES, GROUPS):
             x_raw[j] = load_x_pair(j)
         b2_all = keep.tile([P, D], BF16)
         nc.sync.dma_start(out=b2_all[:], in_=i_b2.partition_broadcast(P))
@@ -96,8 +98,8 @@ def tile_universalknowledgeintegrator_pb_kernel(tc, x, wk, i_w1, i_b1, i_w2, i_b
         w1_scales = keep.tile([P, 2 * PASSES, D], U8, align_bytes=64)
         w2_codes = keep.tile([P, PASSES, D], U32, align_bytes=64)
         w2_scales = keep.tile([P, PASSES, D], U8, align_bytes=64)
-        wk_codes = keep.tile([P, PASSES * B], U32, align_bytes=64)
-        wk_scales = keep.tile([P, PASSES * B], U8, align_bytes=64)
+        wk_codes = keep.tile([P, PASSES, B], U32, align_bytes=64)
+        wk_scales = keep.tile([P, PASSES, B], U8, align_bytes=64)
         g_codes = keep.tile([P, S, PASSES, B], U32, align_bytes=64)
         g_scales = keep.tile([P, S, PASSES, B], U8, align_bytes=64)
 
@@ -160,69 +162,23 @@ def tile_universalknowledgeintegrator_pb_kernel(tc, x, wk, i_w1, i_b1, i_w2, i_b
                         out=bank[:, t, :],
                         lhsT=w1_codes[:, first_pass + c, cols].bitcast(FP8X4),
                         lhsT_scale=w1_scales[:, first_pass + c, cols],
-                        rhs=codes[c].bitcast(FP8X4),
-                        rhs_scale=scales[c],
+                        rhs=codes[:, c, :].bitcast(FP8X4),
+                        rhs_scale=scales[:, c, :],
                         start=(c == 0),
                         stop=(c == PASSES - 1),
                     )
             return bank
 
-        wk_turned = transpose_tile(wk_raw[:])
-        wk_grouped = keep.tile([P, D], BF16, align_bytes=64)
-        regroup_tile(wk_turned, wk_grouped[:].bitcast(F32))
-        b1_turned = psum_t.tile([P, P], BF16, tag="turned")
-        nc.tensor.transpose(b1_turned[:], b1_rows[:], ident_bf16[:])
-
-        grouped_2 = regroup_weight(w1_raw[2])
-        nc.vector.quantize_mx(out=wk_codes[:].bitcast(FP8X4), scales=wk_scales[:], in_=wk_grouped[:])
-        b1_cols = keep.tile([P, D // P], F32)
-        nc.vector.tensor_copy(out=b1_cols[:], in_=b1_turned[:, 0 : D // P])
-        quantise_weight(grouped_2, w1_codes[:, 2, :], w1_scales[:, 2, :], 0)
-        grouped_3 = regroup_weight(w1_raw[3])
-        quantise_weight(grouped_2, w1_codes[:, 2, :], w1_scales[:, 2, :], 1)
-        quantise_weight(grouped_3, w1_codes[:, 3, :], w1_scales[:, 3, :], 0)
-        x_grouped = {0: prepare_x_pair(0)}
-        quantise_weight(grouped_3, w1_codes[:, 3, :], w1_scales[:, 3, :], 1)
-
-        wk_c = [wk_codes[:, c * B : (c + 1) * B] for c in range(PASSES)]
-        wk_s = [wk_scales[:, c * B : (c + 1) * B] for c in range(PASSES)]
-        know_banks = [first_layer_bank(PASSES, half, wk_c, wk_s) for half in range(HALVES)]
-
-        grouped_0 = regroup_weight(w1_raw[0])
-        x_quant = {0: quantise_x_pair(x_grouped[0])}
-        quantise_weight(grouped_0, w1_codes[:, 0, :], w1_scales[:, 0, :], 0)
-        grouped_1 = regroup_weight(w1_raw[1])
         know = keep.tile([P, HALVES, B, PACK], F32)
-        for half in range(HALVES):
-            nc.vector.tensor_tensor(
-                out=know[:, half],
-                in0=know_banks[half][:].rearrange("p t b -> p b t"),
-                in1=b1_cols[:, half * PACK : (half + 1) * PACK].unsqueeze(1).to_broadcast([P, B, PACK]),
-                op=ADD,
-            )
-        quantise_weight(grouped_0, w1_codes[:, 0, :], w1_scales[:, 0, :], 1)
-        quantise_weight(grouped_1, w1_codes[:, 1, :], w1_scales[:, 1, :], 0)
-        x_grouped[1] = prepare_x_pair(1)
-        quantise_weight(grouped_1, w1_codes[:, 1, :], w1_scales[:, 1, :], 1)
 
-        def multiply_tile(j, i):
-            codes, scales = x_quant[j]
-            tile_c = [codes[:, i, c, :] for c in range(PASSES)]
-            tile_s = [scales[:, i, c, :] for c in range(PASSES)]
-            return [first_layer_bank(0, half, tile_c, tile_s) for half in range(HALVES)]
-
-        def add_knowledge(banks):
+        def first_layer_tile(codes, scales, g_grouped):
+            banks = [first_layer_bank(0, half, codes, scales) for half in range(HALVES)]
             pre = g_stage.tile([P, HALVES, B, PACK], F32, tag="pre")
             for half in range(HALVES):
                 nc.vector.tensor_tensor(
                     out=pre[:, half], in0=banks[half][:].rearrange("p t b -> p b t"), in1=know[:, half], op=ADD
                 )
-            return pre
-
-        def gelu_tile(pre, g_grouped, i):
-            nc.scalar.activation(
-                out=g_grouped[:, i * D : (i + 1) * D], in_=pre[:].rearrange("p c b t -> p (c b t)"), func=GELU
-            )
+            nc.scalar.activation(out=g_grouped, in_=pre[:].rearrange("p c b t -> p (c b t)"), func=GELU)
 
         def quantise_g_pair(j, g_grouped):
             tiles = slice(j * PAIR, (j + 1) * PAIR)
@@ -232,31 +188,7 @@ def tile_universalknowledgeintegrator_pb_kernel(tc, x, wk, i_w1, i_b1, i_w2, i_b
                 in_=g_grouped[:],
             )
 
-        g_grouped = {}
-        w2_grouped = {}
-        for j in range(GROUPS):
-            w2_pass = j - FIRST_W2_GROUP
-            if 0 <= w2_pass < PASSES:
-                w2_grouped[w2_pass] = regroup_weight(w2_raw[w2_pass])
-            g_grouped[j] = g_stage.tile([P, PAIR * D], BF16, tag="g_grouped", bufs=2, align_bytes=64, name="g_grouped")
-
-            banks = multiply_tile(j, 0)
-            pre = add_knowledge(banks)
-            if j + 1 < GROUPS:
-                x_quant[j + 1] = quantise_x_pair(x_grouped[j + 1])
-            gelu_tile(pre, g_grouped[j], 0)
-            if j + 2 < GROUPS:
-                x_grouped[j + 2] = prepare_x_pair(j + 2)
-            banks = multiply_tile(j, 1)
-            pre = add_knowledge(banks)
-            gelu_tile(pre, g_grouped[j], 1)
-            if j >= 1:
-                quantise_g_pair(j - 1, g_grouped[j - 1])
-            if 0 <= w2_pass < PASSES:
-                for half in range(HALVES):
-                    quantise_weight(w2_grouped[w2_pass], w2_codes[:, w2_pass, :], w2_scales[:, w2_pass, :], half)
-
-        def finish_tile(s):
+        def second_layer_tile(s):
             z = o_stage.tile([P, D], F32, tag="z")
             for half in range(HALVES):
                 cols = slice(half * BANK, (half + 1) * BANK)
@@ -272,10 +204,63 @@ def tile_universalknowledgeintegrator_pb_kernel(tc, x, wk, i_w1, i_b1, i_w2, i_b
                         stop=(c == PASSES - 1),
                     )
                 nc.vector.tensor_tensor(out=z[:, cols], in0=bank[:], in1=b2_all[:, cols], op=ADD)
-            nc.scalar.activation(out=z[:], in_=z[:], func=TANH)
-            nc.sync.dma_start(out=out[:, s, :], in_=z[:])
+                nc.scalar.activation(out=z[:, cols], in_=z[:, cols], func=TANH)
+                nc.sync.dma_start(out=out[:, s, cols], in_=z[:, cols])
 
-        finish_tile(0)
-        quantise_g_pair(GROUPS - 1, g_grouped[GROUPS - 1])
-        for s in range(1, S):
-            finish_tile(s)
+        grouped_2 = regroup_weight(w1_raw[2])
+        wk_turned = transpose_tile(wk_raw[:])
+        wk_grouped = keep.tile([P, D], BF16, align_bytes=64)
+        regroup_tile(wk_turned, wk_grouped[:].bitcast(F32))
+        b1_turned = psum_t.tile([P, P], BF16, tag="turned")
+        nc.tensor.transpose(b1_turned[:], b1_rows[:], ident_bf16[:])
+        quantise_weight(grouped_2, w1_codes[:, 2, :], w1_scales[:, 2, :], 0)
+        grouped_3 = regroup_weight(w1_raw[3])
+        nc.vector.quantize_mx(
+            out=wk_codes[:].rearrange("p c b -> p (c b)").bitcast(FP8X4),
+            scales=wk_scales[:].rearrange("p c b -> p (c b)"),
+            in_=wk_grouped[:],
+        )
+        b1_cols = keep.tile([P, D // P], F32)
+        nc.vector.tensor_copy(out=b1_cols[:], in_=b1_turned[:, 0 : D // P])
+        quantise_weight(grouped_2, w1_codes[:, 2, :], w1_scales[:, 2, :], 1)
+        quantise_weight(grouped_3, w1_codes[:, 3, :], w1_scales[:, 3, :], 0)
+        x_grouped = {0: prepare_x_pair(0)}
+        quantise_weight(grouped_3, w1_codes[:, 3, :], w1_scales[:, 3, :], 1)
+        know_banks = [first_layer_bank(PASSES, half, wk_codes, wk_scales) for half in range(HALVES)]
+        grouped_0 = regroup_weight(w1_raw[0])
+        x_quant = {0: quantise_x_pair(x_grouped[0])}
+        quantise_weight(grouped_0, w1_codes[:, 0, :], w1_scales[:, 0, :], 0)
+        grouped_1 = regroup_weight(w1_raw[1])
+        for half in range(HALVES):
+            nc.vector.tensor_tensor(
+                out=know[:, half],
+                in0=know_banks[half][:].rearrange("p t b -> p b t"),
+                in1=b1_cols[:, half * PACK : (half + 1) * PACK].unsqueeze(1).to_broadcast([P, B, PACK]),
+                op=ADD,
+            )
+        quantise_weight(grouped_0, w1_codes[:, 0, :], w1_scales[:, 0, :], 1)
+        quantise_weight(grouped_1, w1_codes[:, 1, :], w1_scales[:, 1, :], 0)
+        x_grouped[1] = prepare_x_pair(1)
+        quantise_weight(grouped_1, w1_codes[:, 1, :], w1_scales[:, 1, :], 1)
+
+        g_grouped = {}
+        for j in range(GROUPS + LAG):
+            if j < PASSES:
+                w2_grouped = regroup_weight(w2_raw[j])
+            if j < GROUPS:
+                g_grouped[j] = g_stage.tile([P, PAIR * D], BF16, tag="g_grouped", name="g_grouped", align_bytes=64)
+                codes, scales = x_quant[j]
+                first_layer_tile(codes[:, 0], scales[:, 0], g_grouped[j][:, 0:D])
+                if j + 1 < GROUPS:
+                    x_quant[j + 1] = quantise_x_pair(x_grouped[j + 1])
+                first_layer_tile(codes[:, 1], scales[:, 1], g_grouped[j][:, D : 2 * D])
+                if j + 2 < GROUPS:
+                    x_grouped[j + 2] = prepare_x_pair(j + 2)
+            if 1 <= j <= GROUPS:
+                quantise_g_pair(j - 1, g_grouped[j - 1])
+            if j < PASSES:
+                for half in range(HALVES):
+                    quantise_weight(w2_grouped, w2_codes[:, j, :], w2_scales[:, j, :], half)
+            if j >= LAG:
+                for i in range(PAIR):
+                    second_layer_tile((j - LAG) * PAIR + i)

@@ -24,6 +24,7 @@ PAIR = 2
 GROUPS = S // PAIR
 LAG = 2
 RUN = 4
+EARLY_COLS = 768
 VECTOR_COLS = 512
 
 FLOPS = 2 * (B * S * D * D * 2 + B * D * D)
@@ -35,7 +36,8 @@ def tile_universalknowledgeintegrator_pb_kernel(tc, x, wk, i_w1, i_b1, i_w2, i_b
         ctx.enter_context(tc.manual_schedule())
         keep = ctx.enter_context(tc.tile_pool(name="keep", bufs=1))
         x_in = ctx.enter_context(tc.tile_pool(name="x_in", bufs=GROUPS))
-        w_in = ctx.enter_context(tc.tile_pool(name="w_in", bufs=3 * PASSES))
+        w_half = ctx.enter_context(tc.tile_pool(name="w_half", bufs=2 * PASSES))
+        w_in = ctx.enter_context(tc.tile_pool(name="w_in", bufs=2 * PASSES))
         w_stage = ctx.enter_context(tc.tile_pool(name="w_stage", bufs=3))
         x_stage = ctx.enter_context(tc.tile_pool(name="x_stage", bufs=2))
         x_mx = ctx.enter_context(tc.tile_pool(name="x_mx", bufs=3))
@@ -62,6 +64,17 @@ def tile_universalknowledgeintegrator_pb_kernel(tc, x, wk, i_w1, i_b1, i_w2, i_b
             )
             return raw
 
+        def load_w1_half(c, half):
+            raw = w_half.tile([P, PACK, BANK], BF16, tag="w_half")
+            cols = slice(half * BANK, (half + 1) * BANK)
+            for u in range(2):
+                k0 = c * K_PASS + u * 2 * P
+                nc.sync.dma_start(
+                    out=raw[:, 2 * u : 2 * u + 2, :],
+                    in_=i_w1[k0 : k0 + 2 * P, cols].rearrange("(p e) n -> p e n", e=2),
+                )
+            return raw
+
         def load_w2_pass(c):
             raw = w_in.tile([P, PACK, D], BF16, tag="w_raw")
             nc.sync.dma_start(
@@ -74,14 +87,17 @@ def tile_universalknowledgeintegrator_pb_kernel(tc, x, wk, i_w1, i_b1, i_w2, i_b
             nc.sync.dma_start(out=raw[:], in_=x[:, j * PAIR : (j + 1) * PAIR, :])
             return raw
 
+        w1_halves = {}
         w1_raw = {}
         x_raw = {}
         w2_raw = {}
-        w1_raw[2] = load_w1_pass(2)
+        w1_halves[2, 0] = load_w1_half(2, 0)
         wk_raw = keep.tile([P, D], BF16)
         nc.sync.dma_start(out=wk_raw[:], in_=wk)
+        w1_halves[2, 1] = load_w1_half(2, 1)
         nc.sync.dma_start(out=b1_rows[0 : D // P, :], in_=i_b1.rearrange("(r c) -> r c", c=P))
-        w1_raw[3] = load_w1_pass(3)
+        w1_halves[3, 0] = load_w1_half(3, 0)
+        w1_halves[3, 1] = load_w1_half(3, 1)
         x_raw[0] = load_x_pair(0)
         w1_raw[0] = load_w1_pass(0)
         w1_raw[1] = load_w1_pass(1)
@@ -100,19 +116,19 @@ def tile_universalknowledgeintegrator_pb_kernel(tc, x, wk, i_w1, i_b1, i_w2, i_b
         w2_scales = keep.tile([P, PASSES, D], U8, align_bytes=64)
         wk_codes = keep.tile([P, PASSES, B], U32, align_bytes=64)
         wk_scales = keep.tile([P, PASSES, B], U8, align_bytes=64)
-        g_codes = keep.tile([P, S, PASSES, B], U32, align_bytes=64)
-        g_scales = keep.tile([P, S, PASSES, B], U8, align_bytes=64)
+        g_codes = keep.tile([P, GROUPS, PASSES, PAIR, B], U32, align_bytes=64)
+        g_scales = keep.tile([P, GROUPS, PASSES, PAIR, B], U8, align_bytes=64)
+
+        def regroup_columns(copy, raw, grouped):
+            copy(
+                out=grouped.rearrange("p (c i) t -> p c t i", i=RUN),
+                in_=raw.rearrange("p t (c i) -> p c t i", i=RUN),
+            )
 
         def regroup_weight(raw):
             grouped = w_stage.tile([P, D, PACK], BF16, tag="w_grouped", align_bytes=64)
-            for copy, cols in (
-                (nc.vector.tensor_copy, slice(0, VECTOR_COLS)),
-                (nc.scalar.copy, slice(VECTOR_COLS, D)),
-            ):
-                copy(
-                    out=grouped[:, cols, :].rearrange("p (c i) t -> p c t i", i=RUN),
-                    in_=raw[:, :, cols].rearrange("p t (c i) -> p c t i", i=RUN),
-                )
+            regroup_columns(nc.vector.tensor_copy, raw[:, :, 0:VECTOR_COLS], grouped[:, 0:VECTOR_COLS, :])
+            regroup_columns(nc.scalar.copy, raw[:, :, VECTOR_COLS:D], grouped[:, VECTOR_COLS:D, :])
             return grouped
 
         def quantise_weight(grouped, codes, scales, half):
@@ -131,35 +147,34 @@ def tile_universalknowledgeintegrator_pb_kernel(tc, x, wk, i_w1, i_b1, i_w2, i_b
             return turned
 
         def regroup_tile(turned, grouped_words):
-            nc.scalar.copy(
-                out=grouped_words.rearrange("p (c b u) -> p c b u", c=PASSES, u=2),
-                in_=turned[:].rearrange("p (c u) b -> p c b u", u=2),
-            )
+            nc.scalar.copy(out=grouped_words, in_=turned[:].rearrange("p (c u) b -> p c b u", u=2))
 
         def prepare_x_pair(j):
             grouped = x_stage.tile([P, PAIR * D], BF16, tag="x_grouped", align_bytes=64)
+            words = grouped[:].bitcast(F32).rearrange("p (c i b u) -> p c i b u", c=PASSES, i=PAIR, u=2)
             turned = [transpose_tile(x_raw[j][:, i, :]) for i in range(PAIR)]
             for i in range(PAIR):
-                regroup_tile(turned[i], grouped[:, i * D : (i + 1) * D].bitcast(F32))
+                regroup_tile(turned[i], words[:, :, i])
             return grouped
 
         def quantise_x_pair(grouped):
-            codes = x_mx.tile([P, PAIR, PASSES, B], U32, tag="x_codes", align_bytes=64)
-            scales = x_mx.tile([P, PAIR, PASSES, B], U8, tag="x_scales", align_bytes=64)
+            codes = x_mx.tile([P, PASSES, PAIR * B], U32, tag="x_codes", align_bytes=64)
+            scales = x_mx.tile([P, PASSES, PAIR * B], U8, tag="x_scales", align_bytes=64)
             nc.vector.quantize_mx(
-                out=codes[:].rearrange("p i c b -> p (i c b)").bitcast(FP8X4),
-                scales=scales[:].rearrange("p i c b -> p (i c b)"),
+                out=codes[:].rearrange("p c n -> p (c n)").bitcast(FP8X4),
+                scales=scales[:].rearrange("p c n -> p (c n)"),
                 in_=grouped[:],
             )
             return codes, scales
 
-        def first_layer_bank(first_pass, half, codes, scales):
-            bank = psum_mm.tile([P, PACK, B], F32, tag="bank")
-            for t in range(PACK):
+        def first_layer_bank(first_pass, half, outputs, codes, scales):
+            width = BANK // len(outputs)
+            bank = psum_mm.tile([P, len(outputs), width], F32, tag="bank")
+            for k, t in enumerate(outputs):
                 cols = slice(half * BANK + t * P, half * BANK + (t + 1) * P)
                 for c in range(PASSES):
                     nc.tensor.matmul_mx(
-                        out=bank[:, t, :],
+                        out=bank[:, k, :],
                         lhsT=w1_codes[:, first_pass + c, cols].bitcast(FP8X4),
                         lhsT_scale=w1_scales[:, first_pass + c, cols],
                         rhs=codes[:, c, :].bitcast(FP8X4),
@@ -169,26 +184,33 @@ def tile_universalknowledgeintegrator_pb_kernel(tc, x, wk, i_w1, i_b1, i_w2, i_b
                     )
             return bank
 
-        know = keep.tile([P, HALVES, B, PACK], F32)
+        know = keep.tile([P, HALVES, 2, B, 2], F32)
 
-        def first_layer_tile(codes, scales, g_grouped):
-            banks = [first_layer_bank(0, half, codes, scales) for half in range(HALVES)]
-            pre = g_stage.tile([P, HALVES, B, PACK], F32, tag="pre")
-            for half in range(HALVES):
+        def first_layer_half(half, codes, scales, g_grouped):
+            pre = g_stage.tile([P, 2, PAIR * B, 2], F32, tag="pre")
+            for v in range(2):
+                bank = first_layer_bank(0, half, (2 * v, 2 * v + 1), codes, scales)
                 nc.vector.tensor_tensor(
-                    out=pre[:, half], in0=banks[half][:].rearrange("p t b -> p b t"), in1=know[:, half], op=ADD
+                    out=pre[:, v].rearrange("p (i b) e -> p i b e", i=PAIR),
+                    in0=bank[:].rearrange("p e (i b) -> p i b e", i=PAIR),
+                    in1=know[:, half, v].unsqueeze(1).to_broadcast([P, PAIR, B, 2]),
+                    op=ADD,
                 )
-            nc.scalar.activation(out=g_grouped, in_=pre[:].rearrange("p c b t -> p (c b t)"), func=GELU)
+            nc.scalar.activation(
+                out=g_grouped[:, half * D : (half + 1) * D].rearrange("p (n v e) -> p n v e", v=2, e=2),
+                in_=pre[:].rearrange("p v n e -> p n v e"),
+                func=GELU,
+            )
 
         def quantise_g_pair(j, g_grouped):
-            tiles = slice(j * PAIR, (j + 1) * PAIR)
             nc.vector.quantize_mx(
-                out=g_codes[:, tiles].rearrange("p s c b -> p (s c b)").bitcast(FP8X4),
-                scales=g_scales[:, tiles].rearrange("p s c b -> p (s c b)"),
+                out=g_codes[:, j].rearrange("p c i b -> p (c i b)").bitcast(FP8X4),
+                scales=g_scales[:, j].rearrange("p c i b -> p (c i b)"),
                 in_=g_grouped[:],
             )
 
-        def second_layer_tile(s):
+        def second_layer_tile(j, i):
+            s = j * PAIR + i
             z = o_stage.tile([P, D], F32, tag="z")
             for half in range(HALVES):
                 cols = slice(half * BANK, (half + 1) * BANK)
@@ -196,8 +218,8 @@ def tile_universalknowledgeintegrator_pb_kernel(tc, x, wk, i_w1, i_b1, i_w2, i_b
                 for c in range(PASSES):
                     nc.tensor.matmul_mx(
                         out=bank[:],
-                        lhsT=g_codes[:, s, c, :].bitcast(FP8X4),
-                        lhsT_scale=g_scales[:, s, c, :],
+                        lhsT=g_codes[:, j, c, i, :].bitcast(FP8X4),
+                        lhsT_scale=g_scales[:, j, c, i, :],
                         rhs=w2_codes[:, c, cols].bitcast(FP8X4),
                         rhs_scale=w2_scales[:, c, cols],
                         start=(c == 0),
@@ -207,14 +229,20 @@ def tile_universalknowledgeintegrator_pb_kernel(tc, x, wk, i_w1, i_b1, i_w2, i_b
                 nc.scalar.activation(out=z[:, cols], in_=z[:, cols], func=TANH)
                 nc.sync.dma_start(out=out[:, s, cols], in_=z[:, cols])
 
-        grouped_2 = regroup_weight(w1_raw[2])
+        grouped_2 = w_stage.tile([P, D, PACK], BF16, tag="w_grouped", name="grouped_2", align_bytes=64)
+        regroup_columns(nc.vector.tensor_copy, w1_halves[2, 0][:], grouped_2[:, 0:BANK, :])
         wk_turned = transpose_tile(wk_raw[:])
         wk_grouped = keep.tile([P, D], BF16, align_bytes=64)
-        regroup_tile(wk_turned, wk_grouped[:].bitcast(F32))
+        regroup_tile(wk_turned, wk_grouped[:].bitcast(F32).rearrange("p (c b u) -> p c b u", c=PASSES, u=2))
         b1_turned = psum_t.tile([P, P], BF16, tag="turned")
         nc.tensor.transpose(b1_turned[:], b1_rows[:], ident_bf16[:])
         quantise_weight(grouped_2, w1_codes[:, 2, :], w1_scales[:, 2, :], 0)
-        grouped_3 = regroup_weight(w1_raw[3])
+        more = EARLY_COLS - BANK
+        regroup_columns(nc.vector.tensor_copy, w1_halves[2, 1][:, :, 0:more], grouped_2[:, BANK:EARLY_COLS, :])
+        regroup_columns(nc.scalar.copy, w1_halves[2, 1][:, :, more:BANK], grouped_2[:, EARLY_COLS:D, :])
+        grouped_3 = w_stage.tile([P, D, PACK], BF16, tag="w_grouped", name="grouped_3", align_bytes=64)
+        regroup_columns(nc.vector.tensor_copy, w1_halves[3, 0][:], grouped_3[:, 0:BANK, :])
+        regroup_columns(nc.scalar.copy, w1_halves[3, 1][:], grouped_3[:, BANK:D, :])
         nc.vector.quantize_mx(
             out=wk_codes[:].rearrange("p c b -> p (c b)").bitcast(FP8X4),
             scales=wk_scales[:].rearrange("p c b -> p (c b)"),
@@ -226,7 +254,7 @@ def tile_universalknowledgeintegrator_pb_kernel(tc, x, wk, i_w1, i_b1, i_w2, i_b
         quantise_weight(grouped_3, w1_codes[:, 3, :], w1_scales[:, 3, :], 0)
         x_grouped = {0: prepare_x_pair(0)}
         quantise_weight(grouped_3, w1_codes[:, 3, :], w1_scales[:, 3, :], 1)
-        know_banks = [first_layer_bank(PASSES, half, wk_codes, wk_scales) for half in range(HALVES)]
+        know_banks = [first_layer_bank(PASSES, half, range(PACK), wk_codes, wk_scales) for half in range(HALVES)]
         grouped_0 = regroup_weight(w1_raw[0])
         x_quant = {0: quantise_x_pair(x_grouped[0])}
         quantise_weight(grouped_0, w1_codes[:, 0, :], w1_scales[:, 0, :], 0)
@@ -234,8 +262,11 @@ def tile_universalknowledgeintegrator_pb_kernel(tc, x, wk, i_w1, i_b1, i_w2, i_b
         for half in range(HALVES):
             nc.vector.tensor_tensor(
                 out=know[:, half],
-                in0=know_banks[half][:].rearrange("p t b -> p b t"),
-                in1=b1_cols[:, half * PACK : (half + 1) * PACK].unsqueeze(1).to_broadcast([P, B, PACK]),
+                in0=know_banks[half][:].rearrange("p (v e) b -> p v b e", v=2),
+                in1=b1_cols[:, half * PACK : (half + 1) * PACK]
+                .rearrange("p (v e) -> p v e", v=2)
+                .unsqueeze(2)
+                .to_broadcast([P, 2, B, 2]),
                 op=ADD,
             )
         quantise_weight(grouped_0, w1_codes[:, 0, :], w1_scales[:, 0, :], 1)
@@ -249,11 +280,10 @@ def tile_universalknowledgeintegrator_pb_kernel(tc, x, wk, i_w1, i_b1, i_w2, i_b
                 w2_grouped = regroup_weight(w2_raw[j])
             if j < GROUPS:
                 g_grouped[j] = g_stage.tile([P, PAIR * D], BF16, tag="g_grouped", name="g_grouped", align_bytes=64)
-                codes, scales = x_quant[j]
-                first_layer_tile(codes[:, 0], scales[:, 0], g_grouped[j][:, 0:D])
+                first_layer_half(0, x_quant[j][0], x_quant[j][1], g_grouped[j])
                 if j + 1 < GROUPS:
                     x_quant[j + 1] = quantise_x_pair(x_grouped[j + 1])
-                first_layer_tile(codes[:, 1], scales[:, 1], g_grouped[j][:, D : 2 * D])
+                first_layer_half(1, x_quant[j][0], x_quant[j][1], g_grouped[j])
                 if j + 2 < GROUPS:
                     x_grouped[j + 2] = prepare_x_pair(j + 2)
             if 1 <= j <= GROUPS:
@@ -263,4 +293,4 @@ def tile_universalknowledgeintegrator_pb_kernel(tc, x, wk, i_w1, i_b1, i_w2, i_b
                     quantise_weight(w2_grouped, w2_codes[:, j, :], w2_scales[:, j, :], half)
             if j >= LAG:
                 for i in range(PAIR):
-                    second_layer_tile((j - LAG) * PAIR + i)
+                    second_layer_tile(j - LAG, i)

@@ -25,6 +25,7 @@ GROUPS = S // PAIR
 LAG = 2
 RUN = 4
 EARLY_COLS = 768
+W2_COLS = (256, 512)
 VECTOR_COLS = 512
 
 FLOPS = 2 * (B * S * D * D * 2 + B * D * D)
@@ -36,8 +37,8 @@ def tile_universalknowledgeintegrator_pb_kernel(tc, x, wk, i_w1, i_b1, i_w2, i_b
         ctx.enter_context(tc.manual_schedule())
         keep = ctx.enter_context(tc.tile_pool(name="keep", bufs=1))
         x_in = ctx.enter_context(tc.tile_pool(name="x_in", bufs=GROUPS))
-        w_half = ctx.enter_context(tc.tile_pool(name="w_half", bufs=2 * PASSES))
-        w_in = ctx.enter_context(tc.tile_pool(name="w_in", bufs=2 * PASSES))
+        w_half = ctx.enter_context(tc.tile_pool(name="w_half", bufs=HALVES))
+        w_in = ctx.enter_context(tc.tile_pool(name="w_in", bufs=2 * PASSES + 1))
         w_stage = ctx.enter_context(tc.tile_pool(name="w_stage", bufs=3))
         x_stage = ctx.enter_context(tc.tile_pool(name="x_stage", bufs=2))
         x_mx = ctx.enter_context(tc.tile_pool(name="x_mx", bufs=3))
@@ -96,8 +97,7 @@ def tile_universalknowledgeintegrator_pb_kernel(tc, x, wk, i_w1, i_b1, i_w2, i_b
         nc.sync.dma_start(out=wk_raw[:], in_=wk)
         w1_halves[2, 1] = load_w1_half(2, 1)
         nc.sync.dma_start(out=b1_rows[0 : D // P, :], in_=i_b1.rearrange("(r c) -> r c", c=P))
-        w1_halves[3, 0] = load_w1_half(3, 0)
-        w1_halves[3, 1] = load_w1_half(3, 1)
+        w1_raw[3] = load_w1_pass(3)
         x_raw[0] = load_x_pair(0)
         w1_raw[0] = load_w1_pass(0)
         w1_raw[1] = load_w1_pass(1)
@@ -125,10 +125,16 @@ def tile_universalknowledgeintegrator_pb_kernel(tc, x, wk, i_w1, i_b1, i_w2, i_b
                 in_=raw.rearrange("p t (c i) -> p c t i", i=RUN),
             )
 
+        def regroup_on_vector(raw, grouped, last):
+            regroup_columns(nc.vector.tensor_copy, raw[:, :, 0:last], grouped[:, 0:last, :])
+
+        def regroup_on_scalar(raw, grouped, first):
+            regroup_columns(nc.scalar.copy, raw[:, :, first:D], grouped[:, first:D, :])
+
         def regroup_weight(raw):
             grouped = w_stage.tile([P, D, PACK], BF16, tag="w_grouped", align_bytes=64)
-            regroup_columns(nc.vector.tensor_copy, raw[:, :, 0:VECTOR_COLS], grouped[:, 0:VECTOR_COLS, :])
-            regroup_columns(nc.scalar.copy, raw[:, :, VECTOR_COLS:D], grouped[:, VECTOR_COLS:D, :])
+            regroup_on_scalar(raw, grouped, VECTOR_COLS)
+            regroup_on_vector(raw, grouped, VECTOR_COLS)
             return grouped
 
         def quantise_weight(grouped, codes, scales, half):
@@ -212,9 +218,12 @@ def tile_universalknowledgeintegrator_pb_kernel(tc, x, wk, i_w1, i_b1, i_w2, i_b
         def second_layer_tile(j, i):
             s = j * PAIR + i
             z = o_stage.tile([P, D], F32, tag="z")
-            for half in range(HALVES):
-                cols = slice(half * BANK, (half + 1) * BANK)
-                bank = psum_mm.tile([P, BANK], F32, tag="bank")
+            pieces = [slice(half * BANK, (half + 1) * BANK) for half in range(HALVES)]
+            if s == S - 1:
+                pieces[-1:] = [slice(D - BANK, D - BANK // 2), slice(D - BANK // 2, D)]
+            for cols in pieces:
+                width = cols.stop - cols.start
+                bank = psum_mm.tile([P, width], F32, tag="bank")
                 for c in range(PASSES):
                     nc.tensor.matmul_mx(
                         out=bank[:],
@@ -229,37 +238,10 @@ def tile_universalknowledgeintegrator_pb_kernel(tc, x, wk, i_w1, i_b1, i_w2, i_b
                 nc.scalar.activation(out=z[:, cols], in_=z[:, cols], func=TANH)
                 nc.sync.dma_start(out=out[:, s, cols], in_=z[:, cols])
 
-        grouped_2 = w_stage.tile([P, D, PACK], BF16, tag="w_grouped", name="grouped_2", align_bytes=64)
-        regroup_columns(nc.vector.tensor_copy, w1_halves[2, 0][:], grouped_2[:, 0:BANK, :])
-        wk_turned = transpose_tile(wk_raw[:])
-        wk_grouped = keep.tile([P, D], BF16, align_bytes=64)
-        regroup_tile(wk_turned, wk_grouped[:].bitcast(F32).rearrange("p (c b u) -> p c b u", c=PASSES, u=2))
-        b1_turned = psum_t.tile([P, P], BF16, tag="turned")
-        nc.tensor.transpose(b1_turned[:], b1_rows[:], ident_bf16[:])
-        quantise_weight(grouped_2, w1_codes[:, 2, :], w1_scales[:, 2, :], 0)
-        more = EARLY_COLS - BANK
-        regroup_columns(nc.vector.tensor_copy, w1_halves[2, 1][:, :, 0:more], grouped_2[:, BANK:EARLY_COLS, :])
-        regroup_columns(nc.scalar.copy, w1_halves[2, 1][:, :, more:BANK], grouped_2[:, EARLY_COLS:D, :])
-        grouped_3 = w_stage.tile([P, D, PACK], BF16, tag="w_grouped", name="grouped_3", align_bytes=64)
-        regroup_columns(nc.vector.tensor_copy, w1_halves[3, 0][:], grouped_3[:, 0:BANK, :])
-        regroup_columns(nc.scalar.copy, w1_halves[3, 1][:], grouped_3[:, BANK:D, :])
-        nc.vector.quantize_mx(
-            out=wk_codes[:].rearrange("p c b -> p (c b)").bitcast(FP8X4),
-            scales=wk_scales[:].rearrange("p c b -> p (c b)"),
-            in_=wk_grouped[:],
-        )
-        b1_cols = keep.tile([P, D // P], F32)
-        nc.vector.tensor_copy(out=b1_cols[:], in_=b1_turned[:, 0 : D // P])
-        quantise_weight(grouped_2, w1_codes[:, 2, :], w1_scales[:, 2, :], 1)
-        quantise_weight(grouped_3, w1_codes[:, 3, :], w1_scales[:, 3, :], 0)
-        x_grouped = {0: prepare_x_pair(0)}
-        quantise_weight(grouped_3, w1_codes[:, 3, :], w1_scales[:, 3, :], 1)
-        know_banks = [first_layer_bank(PASSES, half, range(PACK), wk_codes, wk_scales) for half in range(HALVES)]
-        grouped_0 = regroup_weight(w1_raw[0])
-        x_quant = {0: quantise_x_pair(x_grouped[0])}
-        quantise_weight(grouped_0, w1_codes[:, 0, :], w1_scales[:, 0, :], 0)
-        grouped_1 = regroup_weight(w1_raw[1])
-        for half in range(HALVES):
+        def quantise_w1(grouped, c, half):
+            quantise_weight(grouped, w1_codes[:, c, :], w1_scales[:, c, :], half)
+
+        def add_knowledge(half):
             nc.vector.tensor_tensor(
                 out=know[:, half],
                 in0=know_banks[half][:].rearrange("p (v e) b -> p v b e", v=2),
@@ -269,28 +251,75 @@ def tile_universalknowledgeintegrator_pb_kernel(tc, x, wk, i_w1, i_b1, i_w2, i_b
                 .to_broadcast([P, 2, B, 2]),
                 op=ADD,
             )
-        quantise_weight(grouped_0, w1_codes[:, 0, :], w1_scales[:, 0, :], 1)
-        quantise_weight(grouped_1, w1_codes[:, 1, :], w1_scales[:, 1, :], 0)
+
+        grouped_2 = w_stage.tile([P, D, PACK], BF16, tag="w_grouped", name="grouped_2", align_bytes=64)
+        regroup_columns(nc.vector.tensor_copy, w1_halves[2, 0][:], grouped_2[:, 0:BANK, :])
+        wk_turned = transpose_tile(wk_raw[:])
+        wk_grouped = keep.tile([P, D], BF16, align_bytes=64)
+        regroup_tile(wk_turned, wk_grouped[:].bitcast(F32).rearrange("p (c b u) -> p c b u", c=PASSES, u=2))
+        b1_turned = psum_t.tile([P, P], BF16, tag="turned")
+        nc.tensor.transpose(b1_turned[:], b1_rows[:], ident_bf16[:])
+        quantise_w1(grouped_2, 2, 0)
+        more = EARLY_COLS - BANK
+        regroup_columns(nc.vector.tensor_copy, w1_halves[2, 1][:, :, 0:more], grouped_2[:, BANK:EARLY_COLS, :])
+        regroup_columns(nc.scalar.copy, w1_halves[2, 1][:, :, more:BANK], grouped_2[:, EARLY_COLS:D, :])
+        nc.vector.quantize_mx(
+            out=wk_codes[:].rearrange("p c b -> p (c b)").bitcast(FP8X4),
+            scales=wk_scales[:].rearrange("p c b -> p (c b)"),
+            in_=wk_grouped[:],
+        )
+        b1_cols = keep.tile([P, D // P], F32)
+        nc.vector.tensor_copy(out=b1_cols[:], in_=b1_turned[:, 0 : D // P])
+        quantise_w1(grouped_2, 2, 1)
+        grouped_3 = regroup_weight(w1_raw[3])
+        quantise_w1(grouped_3, 3, 0)
+        x_grouped = {0: prepare_x_pair(0)}
+        quantise_w1(grouped_3, 3, 1)
+        know_banks = [first_layer_bank(PASSES, half, range(PACK), wk_codes, wk_scales) for half in range(HALVES)]
+        grouped_0 = regroup_weight(w1_raw[0])
+        x_quant = {0: quantise_x_pair(x_grouped[0])}
+        quantise_w1(grouped_0, 0, 0)
+        add_knowledge(0)
+        grouped_1 = regroup_weight(w1_raw[1])
+        quantise_w1(grouped_0, 0, 1)
+        quantise_w1(grouped_1, 1, 0)
+        add_knowledge(1)
         x_grouped[1] = prepare_x_pair(1)
-        quantise_weight(grouped_1, w1_codes[:, 1, :], w1_scales[:, 1, :], 1)
+        quantise_w1(grouped_1, 1, 1)
+        x_quant[1] = quantise_x_pair(x_grouped[1])
+
+        w2_grouped = [
+            w_stage.tile([P, D, PACK], BF16, tag="w_grouped", name="w2_grouped", align_bytes=64) for c in range(PASSES)
+        ]
+
+        def quantise_w2(c):
+            for half in range(HALVES):
+                quantise_weight(w2_grouped[c], w2_codes[:, c, :], w2_scales[:, c, :], half)
 
         g_grouped = {}
         for j in range(GROUPS + LAG):
-            if j < PASSES:
-                w2_grouped = regroup_weight(w2_raw[j])
+            if j == 0:
+                regroup_on_scalar(w2_raw[0], w2_grouped[0], W2_COLS[0])
             if j < GROUPS:
                 g_grouped[j] = g_stage.tile([P, PAIR * D], BF16, tag="g_grouped", name="g_grouped", align_bytes=64)
                 first_layer_half(0, x_quant[j][0], x_quant[j][1], g_grouped[j])
-                if j + 1 < GROUPS:
+                if j == 0:
+                    regroup_on_vector(w2_raw[0], w2_grouped[0], W2_COLS[0])
+                if 0 < j < GROUPS - 1:
                     x_quant[j + 1] = quantise_x_pair(x_grouped[j + 1])
                 first_layer_half(1, x_quant[j][0], x_quant[j][1], g_grouped[j])
+                if j == 0:
+                    quantise_w2(0)
                 if j + 2 < GROUPS:
                     x_grouped[j + 2] = prepare_x_pair(j + 2)
+                if j == 0:
+                    regroup_on_scalar(w2_raw[1], w2_grouped[1], W2_COLS[1])
+                if j == 1:
+                    regroup_on_vector(w2_raw[1], w2_grouped[1], W2_COLS[1])
             if 1 <= j <= GROUPS:
                 quantise_g_pair(j - 1, g_grouped[j - 1])
-            if j < PASSES:
-                for half in range(HALVES):
-                    quantise_weight(w2_grouped, w2_codes[:, j, :], w2_scales[:, j, :], half)
+            if j == 1:
+                quantise_w2(1)
             if j >= LAG:
                 for i in range(PAIR):
                     second_layer_tile(j - LAG, i)

@@ -9,6 +9,7 @@ U32 = mybir.dt.uint32
 U8 = mybir.dt.uint8
 FP8X4 = mybir.dt.float8_e4m3fn_x4
 ADD = mybir.AluOpType.add
+MULT = mybir.AluOpType.mult
 GELU = mybir.ActivationFunctionType.Gelu
 TANH = mybir.ActivationFunctionType.Tanh
 
@@ -26,6 +27,7 @@ LAG = 2
 RUN = 4
 EARLY_COLS = 768
 W2_COLS = (256, 512)
+ASIDE = 256
 VECTOR_COLS = 512
 
 FLOPS = 2 * (B * S * D * D * 2 + B * D * D)
@@ -125,8 +127,8 @@ def tile_universalknowledgeintegrator_pb_kernel(tc, x, wk, i_w1, i_b1, i_w2, i_b
                 in_=raw.rearrange("p t (c i) -> p c t i", i=RUN),
             )
 
-        def regroup_on_vector(raw, grouped, last):
-            regroup_columns(nc.vector.tensor_copy, raw[:, :, 0:last], grouped[:, 0:last, :])
+        def regroup_on_vector(raw, grouped, last, first=0):
+            regroup_columns(nc.vector.tensor_copy, raw[:, :, first:last], grouped[:, first:last, :])
 
         def regroup_on_scalar(raw, grouped, first):
             regroup_columns(nc.scalar.copy, raw[:, :, first:D], grouped[:, first:D, :])
@@ -136,6 +138,12 @@ def tile_universalknowledgeintegrator_pb_kernel(tc, x, wk, i_w1, i_b1, i_w2, i_b
             regroup_on_scalar(raw, grouped, VECTOR_COLS)
             regroup_on_vector(raw, grouped, VECTOR_COLS)
             return grouped
+
+        def regroup_on_gpsimd(raw, grouped, gate, behind):
+            nc.gpsimd.tensor_copy(out=gate, in_=behind)
+            nc.gpsimd.tensor_scalar(
+                out=grouped, in0=raw.rearrange("p t n -> p n t"), scalar1=1.0, scalar2=0.0, op0=MULT, op1=ADD
+            )
 
         def quantise_weight(grouped, codes, scales, half):
             cols = slice(half * BANK, (half + 1) * BANK)
@@ -296,17 +304,28 @@ def tile_universalknowledgeintegrator_pb_kernel(tc, x, wk, i_w1, i_b1, i_w2, i_b
             for half in range(HALVES):
                 quantise_weight(w2_grouped[c], w2_codes[:, c, :], w2_scales[:, c, :], half)
 
+        gate = keep.tile([P, 4], U32)
+
+        def aside(c, k, behind):
+            cols = slice(k * P, (k + 1) * P)
+            regroup_on_gpsimd(w2_raw[c][:, :, cols], w2_grouped[c][:, cols, :], gate[:, 2 * c + k : 2 * c + k + 1], behind)
+
         g_grouped = {}
         for j in range(GROUPS + LAG):
             if j == 0:
                 regroup_on_scalar(w2_raw[0], w2_grouped[0], W2_COLS[0])
             if j < GROUPS:
                 g_grouped[j] = g_stage.tile([P, PAIR * D], BF16, tag="g_grouped", name="g_grouped", align_bytes=64)
-                first_layer_half(0, x_quant[j][0], x_quant[j][1], g_grouped[j])
                 if j == 0:
-                    regroup_on_vector(w2_raw[0], w2_grouped[0], W2_COLS[0])
+                    aside(0, 0, x_quant[1][0][:, 0, 0:1])
+                    aside(0, 1, x_quant[1][0][:, 0, 0:1])
+                if j == 1:
+                    aside(1, 0, w2_codes[:, 0, D - 1 : D])
+                first_layer_half(0, x_quant[j][0], x_quant[j][1], g_grouped[j])
                 if 0 < j < GROUPS - 1:
                     x_quant[j + 1] = quantise_x_pair(x_grouped[j + 1])
+                if j == 1:
+                    aside(1, 1, x_quant[2][0][:, 0, 0:1])
                 first_layer_half(1, x_quant[j][0], x_quant[j][1], g_grouped[j])
                 if j == 0:
                     quantise_w2(0)
@@ -315,7 +334,7 @@ def tile_universalknowledgeintegrator_pb_kernel(tc, x, wk, i_w1, i_b1, i_w2, i_b
                 if j == 0:
                     regroup_on_scalar(w2_raw[1], w2_grouped[1], W2_COLS[1])
                 if j == 1:
-                    regroup_on_vector(w2_raw[1], w2_grouped[1], W2_COLS[1])
+                    regroup_on_vector(w2_raw[1], w2_grouped[1], W2_COLS[1], ASIDE)
             if 1 <= j <= GROUPS:
                 quantise_g_pair(j - 1, g_grouped[j - 1])
             if j == 1:

@@ -26,9 +26,8 @@ GROUPS = S // PAIR
 LAG = 2
 RUN = 4
 EARLY_COLS = 768
-W2_COLS = (256, 512)
-ASIDE = 256
-VECTOR_COLS = 512
+SECOND_HALF_READY = 4
+VECTOR_COLS = {3: 512, 0: 384, 1: 512}
 
 FLOPS = 2 * (B * S * D * D * 2 + B * D * D)
 
@@ -38,14 +37,16 @@ def tile_universalknowledgeintegrator_pb_kernel(tc, x, wk, i_w1, i_b1, i_w2, i_b
     with ExitStack() as ctx:
         ctx.enter_context(tc.manual_schedule())
         keep = ctx.enter_context(tc.tile_pool(name="keep", bufs=1))
-        x_in = ctx.enter_context(tc.tile_pool(name="x_in", bufs=GROUPS))
+        x_in = ctx.enter_context(tc.tile_pool(name="x_in", bufs=GROUPS - 2))
         w_half = ctx.enter_context(tc.tile_pool(name="w_half", bufs=HALVES))
-        w_in = ctx.enter_context(tc.tile_pool(name="w_in", bufs=2 * PASSES + 1))
+        w2_in = ctx.enter_context(tc.tile_pool(name="w2_in", bufs=HALVES * PASSES))
+        w_in = ctx.enter_context(tc.tile_pool(name="w_in", bufs=2 * PASSES - 1))
+        w2_stage = ctx.enter_context(tc.tile_pool(name="w2_stage", bufs=HALVES * PASSES))
         w_stage = ctx.enter_context(tc.tile_pool(name="w_stage", bufs=3))
         x_stage = ctx.enter_context(tc.tile_pool(name="x_stage", bufs=2))
         x_mx = ctx.enter_context(tc.tile_pool(name="x_mx", bufs=3))
         g_stage = ctx.enter_context(tc.tile_pool(name="g_stage", bufs=3))
-        o_stage = ctx.enter_context(tc.tile_pool(name="o_stage", bufs=5))
+        o_stage = ctx.enter_context(tc.tile_pool(name="o_stage", bufs=12))
         psum_t = ctx.enter_context(tc.psum_pool(name="psum_t", bufs=PAIR))
         psum_mm = ctx.enter_context(tc.psum_pool(name="psum_mm", bufs=PSUM_BANKS - PAIR))
 
@@ -78,10 +79,11 @@ def tile_universalknowledgeintegrator_pb_kernel(tc, x, wk, i_w1, i_b1, i_w2, i_b
                 )
             return raw
 
-        def load_w2_pass(c):
-            raw = w_in.tile([P, PACK, D], BF16, tag="w_raw")
+        def load_w2_half(c, half):
+            raw = w2_in.tile([P, PACK, BANK], BF16, tag="w2_raw")
+            cols = slice(half * BANK, (half + 1) * BANK)
             nc.sync.dma_start(
-                out=raw[:], in_=i_w2[c * K_PASS : (c + 1) * K_PASS, :].rearrange("(t p) n -> p t n", p=P)
+                out=raw[:], in_=i_w2[c * K_PASS : (c + 1) * K_PASS, cols].rearrange("(t p) n -> p t n", p=P)
             )
             return raw
 
@@ -105,8 +107,10 @@ def tile_universalknowledgeintegrator_pb_kernel(tc, x, wk, i_w1, i_b1, i_w2, i_b
         w1_raw[1] = load_w1_pass(1)
         x_raw[1] = load_x_pair(1)
         for c in range(PASSES):
-            w2_raw[c] = load_w2_pass(c)
+            w2_raw[c, 0] = load_w2_half(c, 0)
+        for c in range(PASSES):
             x_raw[2 + c] = load_x_pair(2 + c)
+            w2_raw[c, 1] = load_w2_half(c, 1)
         for j in range(2 + PASSES, GROUPS):
             x_raw[j] = load_x_pair(j)
         b2_all = keep.tile([P, D], BF16)
@@ -127,16 +131,12 @@ def tile_universalknowledgeintegrator_pb_kernel(tc, x, wk, i_w1, i_b1, i_w2, i_b
                 in_=raw.rearrange("p t (c i) -> p c t i", i=RUN),
             )
 
-        def regroup_on_vector(raw, grouped, last, first=0):
-            regroup_columns(nc.vector.tensor_copy, raw[:, :, first:last], grouped[:, first:last, :])
-
-        def regroup_on_scalar(raw, grouped, first):
-            regroup_columns(nc.scalar.copy, raw[:, :, first:D], grouped[:, first:D, :])
-
-        def regroup_weight(raw):
+        def regroup_weight(raw, vector_cols):
             grouped = w_stage.tile([P, D, PACK], BF16, tag="w_grouped", align_bytes=64)
-            regroup_on_scalar(raw, grouped, VECTOR_COLS)
-            regroup_on_vector(raw, grouped, VECTOR_COLS)
+            for first, last in ((vector_cols, BANK), (BANK, D)):
+                if first < last:
+                    regroup_columns(nc.scalar.copy, raw[:, :, first:last], grouped[:, first:last, :])
+            regroup_columns(nc.vector.tensor_copy, raw[:, :, 0:vector_cols], grouped[:, 0:vector_cols, :])
             return grouped
 
         def regroup_on_gpsimd(raw, grouped, gate, behind):
@@ -223,28 +223,46 @@ def tile_universalknowledgeintegrator_pb_kernel(tc, x, wk, i_w1, i_b1, i_w2, i_b
                 in_=g_grouped[:],
             )
 
-        def second_layer_tile(j, i):
-            s = j * PAIR + i
-            z = o_stage.tile([P, D], F32, tag="z")
-            pieces = [slice(half * BANK, (half + 1) * BANK) for half in range(HALVES)]
-            if s == S - 1:
-                pieces[-1:] = [slice(D - BANK, D - BANK // 2), slice(D - BANK // 2, D)]
-            for cols in pieces:
-                width = cols.stop - cols.start
-                bank = psum_mm.tile([P, width], F32, tag="bank")
-                for c in range(PASSES):
-                    nc.tensor.matmul_mx(
-                        out=bank[:],
-                        lhsT=g_codes[:, j, c, i, :].bitcast(FP8X4),
-                        lhsT_scale=g_scales[:, j, c, i, :],
-                        rhs=w2_codes[:, c, cols].bitcast(FP8X4),
-                        rhs_scale=w2_scales[:, c, cols],
-                        start=(c == 0),
-                        stop=(c == PASSES - 1),
-                    )
-                nc.vector.tensor_tensor(out=z[:, cols], in0=bank[:], in1=b2_all[:, cols], op=ADD)
-                nc.scalar.activation(out=z[:, cols], in_=z[:, cols], func=TANH)
-                nc.sync.dma_start(out=out[:, s, cols], in_=z[:, cols])
+        def second_layer_product(bank, j, i, cols):
+            for c in range(PASSES):
+                nc.tensor.matmul_mx(
+                    out=bank[:],
+                    lhsT=g_codes[:, j, c, i, :].bitcast(FP8X4),
+                    lhsT_scale=g_scales[:, j, c, i, :],
+                    rhs=w2_codes[:, c, cols].bitcast(FP8X4),
+                    rhs_scale=w2_scales[:, c, cols],
+                    start=(c == 0),
+                    stop=(c == PASSES - 1),
+                )
+
+        def finish(z, j, i, cols):
+            nc.scalar.activation(out=z, in_=z, func=TANH)
+            nc.sync.dma_start(out=out[:, j * PAIR + i, cols], in_=z)
+
+        def half_columns(half):
+            return slice(half * BANK, (half + 1) * BANK)
+
+        def second_layer_half(j, half, tiles):
+            for i in tiles:
+                pieces = [half_columns(half)]
+                if j == GROUPS - 1 and half == HALVES - 1 and i == PAIR - 1:
+                    pieces = [slice(D - BANK, D - BANK // 2), slice(D - BANK // 2, D)]
+                z = o_stage.tile([P, BANK], F32, tag="z", name="z")
+                for cols in pieces:
+                    bank = psum_mm.tile([P, cols.stop - cols.start], F32, tag="bank", name="bank")
+                    second_layer_product(bank, j, i, cols)
+                    part = z[:, cols.start - half * BANK : cols.stop - half * BANK]
+                    nc.vector.tensor_tensor(out=part, in0=bank[:], in1=b2_all[:, cols], op=ADD)
+                    finish(part, j, i, cols)
+
+        def add_on_gpsimd(j, half, i):
+            cols = half_columns(half)
+            bank = psum_t.tile([P, BANK], F32, tag="turned", name="bank_aside")
+            second_layer_product(bank, j, i, cols)
+            z = o_stage.tile([P, BANK], F32, tag="z", name="z")
+            nc.scalar.copy(out=z[:], in_=bank[:])
+            nc.gpsimd.tensor_tensor(out=z[:], in0=z[:], in1=b2_all[:, cols], op=ADD)
+            return z
 
         def quantise_w1(grouped, c, half):
             quantise_weight(grouped, w1_codes[:, c, :], w1_scales[:, c, :], half)
@@ -279,66 +297,91 @@ def tile_universalknowledgeintegrator_pb_kernel(tc, x, wk, i_w1, i_b1, i_w2, i_b
         b1_cols = keep.tile([P, D // P], F32)
         nc.vector.tensor_copy(out=b1_cols[:], in_=b1_turned[:, 0 : D // P])
         quantise_w1(grouped_2, 2, 1)
-        grouped_3 = regroup_weight(w1_raw[3])
+        grouped_3 = regroup_weight(w1_raw[3], VECTOR_COLS[3])
         quantise_w1(grouped_3, 3, 0)
         x_grouped = {0: prepare_x_pair(0)}
         quantise_w1(grouped_3, 3, 1)
         know_banks = [first_layer_bank(PASSES, half, range(PACK), wk_codes, wk_scales) for half in range(HALVES)]
-        grouped_0 = regroup_weight(w1_raw[0])
+        grouped_0 = regroup_weight(w1_raw[0], VECTOR_COLS[0])
         x_quant = {0: quantise_x_pair(x_grouped[0])}
         quantise_w1(grouped_0, 0, 0)
         add_knowledge(0)
-        grouped_1 = regroup_weight(w1_raw[1])
+        grouped_1 = regroup_weight(w1_raw[1], VECTOR_COLS[1])
         quantise_w1(grouped_0, 0, 1)
         quantise_w1(grouped_1, 1, 0)
         add_knowledge(1)
-        x_grouped[1] = prepare_x_pair(1)
         quantise_w1(grouped_1, 1, 1)
-        x_quant[1] = quantise_x_pair(x_grouped[1])
+        x_grouped[1] = prepare_x_pair(1)
 
-        w2_grouped = [
-            w_stage.tile([P, D, PACK], BF16, tag="w_grouped", name="w2_grouped", align_bytes=64) for c in range(PASSES)
-        ]
+        w2_grouped = {
+            (c, half): w2_stage.tile([P, BANK, PACK], BF16, tag="w2_grouped", name="w2_grouped", align_bytes=64)
+            for half in range(HALVES)
+            for c in range(PASSES)
+        }
+        pieces = [(c, half, k) for half in range(HALVES) for c in range(PASSES) for k in range(2 + 2 * half)]
+        gate = keep.tile([P, len(pieces)], U32)
 
-        def quantise_w2(c):
-            for half in range(HALVES):
-                quantise_weight(w2_grouped[c], w2_codes[:, c, :], w2_scales[:, c, :], half)
+        def run_aside(count, behind):
+            for turn in range(count):
+                piece = pieces[0]
+                pieces.remove(piece)
+                c, half, k = piece
+                cols = slice(k * P, (k + 1) * P)
+                left = len(pieces)
+                regroup_on_gpsimd(
+                    w2_raw[c, half][:, :, cols], w2_grouped[c, half][:, cols, :], gate[:, left : left + 1], behind
+                )
 
-        gate = keep.tile([P, 4], U32)
+        def regroup_w2_on_scalar(c):
+            cols = slice(2 * P, BANK)
+            regroup_columns(nc.scalar.copy, w2_raw[c, 0][:, :, cols], w2_grouped[c, 0][:, cols, :])
 
-        def aside(c, k, behind):
-            cols = slice(k * P, (k + 1) * P)
-            regroup_on_gpsimd(w2_raw[c][:, :, cols], w2_grouped[c][:, cols, :], gate[:, 2 * c + k : 2 * c + k + 1], behind)
+        def quantise_w2(c, half):
+            cols = slice(half * BANK, (half + 1) * BANK)
+            nc.vector.quantize_mx(
+                out=w2_codes[:, c, cols].bitcast(FP8X4),
+                scales=w2_scales[:, c, cols],
+                in_=w2_grouped[c, half][:].rearrange("p n t -> p (n t)"),
+            )
 
         g_grouped = {}
         for j in range(GROUPS + LAG):
             if j == 0:
-                regroup_on_scalar(w2_raw[0], w2_grouped[0], W2_COLS[0])
+                run_aside(2, w1_codes[:, 1, D - 1 : D])
+                regroup_w2_on_scalar(0)
+            if 1 <= j <= PASSES:
+                run_aside(1, w2_codes[:, j - 1, BANK - 1 : BANK])
             if j < GROUPS:
                 g_grouped[j] = g_stage.tile([P, PAIR * D], BF16, tag="g_grouped", name="g_grouped", align_bytes=64)
-                if j == 0:
-                    aside(0, 0, x_quant[1][0][:, 0, 0:1])
-                    aside(0, 1, x_quant[1][0][:, 0, 0:1])
-                if j == 1:
-                    aside(1, 0, w2_codes[:, 0, D - 1 : D])
                 first_layer_half(0, x_quant[j][0], x_quant[j][1], g_grouped[j])
                 if 0 < j < GROUPS - 1:
                     x_quant[j + 1] = quantise_x_pair(x_grouped[j + 1])
-                if j == 1:
-                    aside(1, 1, x_quant[2][0][:, 0, 0:1])
+                    if j <= SECOND_HALF_READY:
+                        run_aside(1, x_quant[j + 1][0][:, 0, 0:1])
                 first_layer_half(1, x_quant[j][0], x_quant[j][1], g_grouped[j])
                 if j == 0:
-                    quantise_w2(0)
+                    x_quant[1] = quantise_x_pair(x_grouped[1])
                 if j + 2 < GROUPS:
                     x_grouped[j + 2] = prepare_x_pair(j + 2)
                 if j == 0:
-                    regroup_on_scalar(w2_raw[1], w2_grouped[1], W2_COLS[1])
-                if j == 1:
-                    regroup_on_vector(w2_raw[1], w2_grouped[1], W2_COLS[1], ASIDE)
+                    regroup_w2_on_scalar(1)
             if 1 <= j <= GROUPS:
                 quantise_g_pair(j - 1, g_grouped[j - 1])
-            if j == 1:
-                quantise_w2(1)
+            if j < PASSES:
+                quantise_w2(j, 0)
+            if PASSES <= j < SECOND_HALF_READY:
+                run_aside(2, g_codes[:, j - 1, 0, 0, 0:1])
+            if j == SECOND_HALF_READY:
+                for c in range(PASSES):
+                    quantise_w2(c, 1)
+            late = 2 * (j - SECOND_HALF_READY - 1)
+            catch_up = [p for p in (late, late + 1) if p >= 0] if j < GROUPS else [j - LAG]
+            over_gpsimd = GROUPS - 2 <= j < GROUPS
+            if over_gpsimd:
+                z = add_on_gpsimd(late, 1, 0)
             if j >= LAG:
-                for i in range(PAIR):
-                    second_layer_tile(j - LAG, i)
+                second_layer_half(j - LAG, 0, range(PAIR))
+            for p in catch_up:
+                second_layer_half(p, 1, range(1 if over_gpsimd and p == late else 0, PAIR))
+            if over_gpsimd:
+                finish(z[:], late, 0, half_columns(1))

@@ -39,7 +39,7 @@ def tile_universalknowledgeintegrator_pb_kernel(tc, x, wk, i_w1, i_b1, i_w2, i_b
         keep = ctx.enter_context(tc.tile_pool(name="keep", bufs=1))
         x_in = ctx.enter_context(tc.tile_pool(name="x_in", bufs=GROUPS - 2))
         w_half = ctx.enter_context(tc.tile_pool(name="w_half", bufs=HALVES))
-        w2_in = ctx.enter_context(tc.tile_pool(name="w2_in", bufs=HALVES * PASSES))
+        w2_in = ctx.enter_context(tc.tile_pool(name="w2_in", bufs=PASSES))
         w_in = ctx.enter_context(tc.tile_pool(name="w_in", bufs=2 * PASSES - 1))
         w2_stage = ctx.enter_context(tc.tile_pool(name="w2_stage", bufs=HALVES * PASSES))
         w_stage = ctx.enter_context(tc.tile_pool(name="w_stage", bufs=3))
@@ -79,11 +79,10 @@ def tile_universalknowledgeintegrator_pb_kernel(tc, x, wk, i_w1, i_b1, i_w2, i_b
                 )
             return raw
 
-        def load_w2_half(c, half):
-            raw = w2_in.tile([P, PACK, BANK], BF16, tag="w2_raw")
-            cols = slice(half * BANK, (half + 1) * BANK)
+        def load_w2_pass(c):
+            raw = w2_in.tile([P, PACK, D], BF16, tag="w2_raw")
             nc.sync.dma_start(
-                out=raw[:], in_=i_w2[c * K_PASS : (c + 1) * K_PASS, cols].rearrange("(t p) n -> p t n", p=P)
+                out=raw[:], in_=i_w2[c * K_PASS : (c + 1) * K_PASS, :].rearrange("(t p) n -> p t n", p=P)
             )
             return raw
 
@@ -107,10 +106,8 @@ def tile_universalknowledgeintegrator_pb_kernel(tc, x, wk, i_w1, i_b1, i_w2, i_b
         w1_raw[1] = load_w1_pass(1)
         x_raw[1] = load_x_pair(1)
         for c in range(PASSES):
-            w2_raw[c, 0] = load_w2_half(c, 0)
-        for c in range(PASSES):
+            w2_raw[c] = load_w2_pass(c)
             x_raw[2 + c] = load_x_pair(2 + c)
-            w2_raw[c, 1] = load_w2_half(c, 1)
         for j in range(2 + PASSES, GROUPS):
             x_raw[j] = load_x_pair(j)
         b2_all = keep.tile([P, D], BF16)
@@ -326,15 +323,16 @@ def tile_universalknowledgeintegrator_pb_kernel(tc, x, wk, i_w1, i_b1, i_w2, i_b
                 piece = pieces[0]
                 pieces.remove(piece)
                 c, half, k = piece
+                source = slice(half * BANK + k * P, half * BANK + (k + 1) * P)
                 cols = slice(k * P, (k + 1) * P)
                 left = len(pieces)
                 regroup_on_gpsimd(
-                    w2_raw[c, half][:, :, cols], w2_grouped[c, half][:, cols, :], gate[:, left : left + 1], behind
+                    w2_raw[c][:, :, source], w2_grouped[c, half][:, cols, :], gate[:, left : left + 1], behind
                 )
 
         def regroup_w2_on_scalar(c):
             cols = slice(2 * P, BANK)
-            regroup_columns(nc.scalar.copy, w2_raw[c, 0][:, :, cols], w2_grouped[c, 0][:, cols, :])
+            regroup_columns(nc.scalar.copy, w2_raw[c][:, :, cols], w2_grouped[c, 0][:, cols, :])
 
         def quantise_w2(c, half):
             cols = slice(half * BANK, (half + 1) * BANK)
@@ -349,28 +347,23 @@ def tile_universalknowledgeintegrator_pb_kernel(tc, x, wk, i_w1, i_b1, i_w2, i_b
             if j == 0:
                 run_aside(2, w1_codes[:, 1, D - 1 : D])
                 regroup_w2_on_scalar(0)
-            if 1 <= j <= PASSES:
-                run_aside(1, w2_codes[:, j - 1, BANK - 1 : BANK])
             if j < GROUPS:
                 g_grouped[j] = g_stage.tile([P, PAIR * D], BF16, tag="g_grouped", name="g_grouped", align_bytes=64)
-                first_layer_half(0, x_quant[j][0], x_quant[j][1], g_grouped[j])
-                if 0 < j < GROUPS - 1:
-                    x_quant[j + 1] = quantise_x_pair(x_grouped[j + 1])
-                    if j <= SECOND_HALF_READY:
-                        run_aside(1, x_quant[j + 1][0][:, 0, 0:1])
-                first_layer_half(1, x_quant[j][0], x_quant[j][1], g_grouped[j])
-                if j == 0:
-                    x_quant[1] = quantise_x_pair(x_grouped[1])
-                if j + 2 < GROUPS:
-                    x_grouped[j + 2] = prepare_x_pair(j + 2)
-                if j == 0:
-                    regroup_w2_on_scalar(1)
+                for half in range(HALVES):
+                    first_layer_half(half, x_quant[j][0], x_quant[j][1], g_grouped[j])
+            if j + 1 < GROUPS:
+                x_quant[j + 1] = quantise_x_pair(x_grouped[j + 1])
+            if j + 2 < GROUPS:
+                x_grouped[j + 2] = prepare_x_pair(j + 2)
+            if j == 0:
+                regroup_w2_on_scalar(1)
             if 1 <= j <= GROUPS:
                 quantise_g_pair(j - 1, g_grouped[j - 1])
             if j < PASSES:
                 quantise_w2(j, 0)
-            if PASSES <= j < SECOND_HALF_READY:
-                run_aside(2, g_codes[:, j - 1, 0, 0, 0:1])
+                run_aside(2, w2_codes[:, j, BANK - 1 : BANK])
+            elif j < SECOND_HALF_READY:
+                run_aside(3, g_codes[:, j - 1, 0, 0, 0:1])
             if j == SECOND_HALF_READY:
                 for c in range(PASSES):
                     quantise_w2(c, 1)

@@ -136,8 +136,7 @@ def tile_universalknowledgeintegrator_pb_kernel(tc, x, wk, i_w1, i_b1, i_w2, i_b
             regroup_columns(nc.vector.tensor_copy, raw[:, :, 0:vector_cols], grouped[:, 0:vector_cols, :])
             return grouped
 
-        def regroup_on_gpsimd(raw, grouped, gate, behind):
-            nc.gpsimd.tensor_copy(out=gate, in_=behind)
+        def regroup_on_gpsimd(raw, grouped):
             nc.gpsimd.tensor_scalar(
                 out=grouped, in0=raw.rearrange("p t n -> p n t"), scalar1=1.0, scalar2=0.0, op0=MULT, op1=ADD
             )
@@ -319,16 +318,15 @@ def tile_universalknowledgeintegrator_pb_kernel(tc, x, wk, i_w1, i_b1, i_w2, i_b
         gate = keep.tile([P, len(pieces)], U32)
 
         def run_aside(count, behind):
+            left = len(pieces)
+            nc.gpsimd.tensor_copy(out=gate[:, left - 1 : left], in_=behind)
             for turn in range(count):
                 piece = pieces[0]
                 pieces.remove(piece)
                 c, half, k = piece
                 source = slice(half * BANK + k * P, half * BANK + (k + 1) * P)
                 cols = slice(k * P, (k + 1) * P)
-                left = len(pieces)
-                regroup_on_gpsimd(
-                    w2_raw[c][:, :, source], w2_grouped[c, half][:, cols, :], gate[:, left : left + 1], behind
-                )
+                regroup_on_gpsimd(w2_raw[c][:, :, source], w2_grouped[c, half][:, cols, :])
 
         def regroup_w2_on_scalar(c):
             cols = slice(2 * P, BANK)
@@ -369,12 +367,11 @@ def tile_universalknowledgeintegrator_pb_kernel(tc, x, wk, i_w1, i_b1, i_w2, i_b
                     quantise_w2(c, 1)
             late = 2 * (j - SECOND_HALF_READY - 1)
             catch_up = [p for p in (late, late + 1) if p >= 0] if j < GROUPS else [j - LAG]
-            over_gpsimd = GROUPS - 2 <= j < GROUPS
-            if over_gpsimd:
-                z = add_on_gpsimd(late, 1, 0)
+            over_gpsimd = catch_up if j == GROUPS - 2 else []
+            aside = [add_on_gpsimd(p, 1, 0) for p in over_gpsimd]
             if j >= LAG:
                 second_layer_half(j - LAG, 0, range(PAIR))
             for p in catch_up:
-                second_layer_half(p, 1, range(1 if over_gpsimd and p == late else 0, PAIR))
-            if over_gpsimd:
-                finish(z[:], late, 0, half_columns(1))
+                second_layer_half(p, 1, range(1 if over_gpsimd else 0, PAIR))
+            for z, p in zip(aside, over_gpsimd):
+                finish(z[:], p, 0, half_columns(1))

from contextlib import ExitStack

import concourse.mybir as mybir
from concourse.masks import make_identity

F32 = mybir.dt.float32
BF16 = mybir.dt.bfloat16
U32 = mybir.dt.uint32
U8 = mybir.dt.uint8
FP8X4 = mybir.dt.float8_e4m3fn_x4
ADD = mybir.AluOpType.add
MULT = mybir.AluOpType.mult
GELU = mybir.ActivationFunctionType.Gelu
TANH = mybir.ActivationFunctionType.Tanh

P = 128
PACK = 4
K_PASS = P * PACK
B, S, D = 128, 16, 1024
PASSES = D // K_PASS
BANK = 512
HALVES = D // BANK
PSUM_BANKS = 8
PAIR = 2
GROUPS = S // PAIR
LAG = 2
RUN = 4
EARLY_COLS = 768
SECOND_HALF_READY = 4
VECTOR_COLS = {3: 512, 0: 384, 1: 512}

FLOPS = 2 * (B * S * D * D * 2 + B * D * D)


def tile_universalknowledgeintegrator_pb_kernel(tc, x, wk, i_w1, i_b1, i_w2, i_b2, out):
    nc = tc.nc
    with ExitStack() as ctx:
        ctx.enter_context(tc.manual_schedule())
        keep = ctx.enter_context(tc.tile_pool(name="keep", bufs=1))
        x_in = ctx.enter_context(tc.tile_pool(name="x_in", bufs=GROUPS - 2))
        w_half = ctx.enter_context(tc.tile_pool(name="w_half", bufs=HALVES))
        w2_in = ctx.enter_context(tc.tile_pool(name="w2_in", bufs=PASSES))
        w_in = ctx.enter_context(tc.tile_pool(name="w_in", bufs=2 * PASSES - 1))
        w2_stage = ctx.enter_context(tc.tile_pool(name="w2_stage", bufs=HALVES * PASSES))
        w_stage = ctx.enter_context(tc.tile_pool(name="w_stage", bufs=3))
        x_stage = ctx.enter_context(tc.tile_pool(name="x_stage", bufs=2))
        x_mx = ctx.enter_context(tc.tile_pool(name="x_mx", bufs=3))
        g_stage = ctx.enter_context(tc.tile_pool(name="g_stage", bufs=3))
        o_stage = ctx.enter_context(tc.tile_pool(name="o_stage", bufs=12))
        psum_t = ctx.enter_context(tc.psum_pool(name="psum_t", bufs=PAIR))
        psum_mm = ctx.enter_context(tc.psum_pool(name="psum_mm", bufs=PSUM_BANKS - PAIR))

        warm = keep.tile([P, 1], F32)
        nc.vector.memset(warm[:], 0.0)
        nc.scalar.activation(out=warm[:], in_=warm[:], func=GELU)
        ident_f32 = keep.tile([P, P], F32)
        make_identity(nc, ident_f32[:])
        ident_bf16 = keep.tile([P, P], BF16)
        make_identity(nc, ident_bf16[:])
        b1_rows = keep.tile([P, P], BF16)
        nc.vector.memset(b1_rows[:], 0.0)

        def load_w1_pass(c):
            raw = w_in.tile([P, PACK, D], BF16, tag="w_raw")
            nc.sync.dma_start(
                out=raw[:].rearrange("p (u e) n -> p u (e n)", u=2),
                in_=i_w1[c * K_PASS : (c + 1) * K_PASS, :].rearrange("(u p e) n -> p u (e n)", u=2, e=2),
            )
            return raw

        def load_w1_half(c, half):
            raw = w_half.tile([P, PACK, BANK], BF16, tag="w_half")
            cols = slice(half * BANK, (half + 1) * BANK)
            for u in range(2):
                k0 = c * K_PASS + u * 2 * P
                nc.sync.dma_start(
                    out=raw[:, 2 * u : 2 * u + 2, :],
                    in_=i_w1[k0 : k0 + 2 * P, cols].rearrange("(p e) n -> p e n", e=2),
                )
            return raw

        def load_w2_pass(c):
            raw = w2_in.tile([P, PACK, D], BF16, tag="w2_raw")
            nc.sync.dma_start(
                out=raw[:], in_=i_w2[c * K_PASS : (c + 1) * K_PASS, :].rearrange("(t p) n -> p t n", p=P)
            )
            return raw

        def load_x_pair(j):
            raw = x_in.tile([P, PAIR, D], BF16, tag="x_raw")
            nc.sync.dma_start(out=raw[:], in_=x[:, j * PAIR : (j + 1) * PAIR, :])
            return raw

        w1_halves = {}
        w1_raw = {}
        x_raw = {}
        w2_raw = {}
        w1_halves[2, 0] = load_w1_half(2, 0)
        wk_raw = keep.tile([P, D], BF16)
        nc.sync.dma_start(out=wk_raw[:], in_=wk)
        w1_halves[2, 1] = load_w1_half(2, 1)
        nc.sync.dma_start(out=b1_rows[0 : D // P, :], in_=i_b1.rearrange("(r c) -> r c", c=P))
        w1_raw[3] = load_w1_pass(3)
        x_raw[0] = load_x_pair(0)
        w1_raw[0] = load_w1_pass(0)
        w1_raw[1] = load_w1_pass(1)
        x_raw[1] = load_x_pair(1)
        for c in range(PASSES):
            w2_raw[c] = load_w2_pass(c)
            x_raw[2 + c] = load_x_pair(2 + c)
        for j in range(2 + PASSES, GROUPS):
            x_raw[j] = load_x_pair(j)
        b2_all = keep.tile([P, D], BF16)
        nc.sync.dma_start(out=b2_all[:], in_=i_b2.partition_broadcast(P))

        w1_codes = keep.tile([P, 2 * PASSES, D], U32, align_bytes=64)
        w1_scales = keep.tile([P, 2 * PASSES, D], U8, align_bytes=64)
        w2_codes = keep.tile([P, PASSES, D], U32, align_bytes=64)
        w2_scales = keep.tile([P, PASSES, D], U8, align_bytes=64)
        wk_codes = keep.tile([P, PASSES, B], U32, align_bytes=64)
        wk_scales = keep.tile([P, PASSES, B], U8, align_bytes=64)
        g_codes = keep.tile([P, GROUPS, PASSES, PAIR, B], U32, align_bytes=64)
        g_scales = keep.tile([P, GROUPS, PASSES, PAIR, B], U8, align_bytes=64)

        def regroup_columns(copy, raw, grouped):
            copy(
                out=grouped.rearrange("p (c i) t -> p c t i", i=RUN),
                in_=raw.rearrange("p t (c i) -> p c t i", i=RUN),
            )

        def regroup_weight(raw, vector_cols):
            grouped = w_stage.tile([P, D, PACK], BF16, tag="w_grouped", align_bytes=64)
            for first, last in ((vector_cols, BANK), (BANK, D)):
                if first < last:
                    regroup_columns(nc.scalar.copy, raw[:, :, first:last], grouped[:, first:last, :])
            regroup_columns(nc.vector.tensor_copy, raw[:, :, 0:vector_cols], grouped[:, 0:vector_cols, :])
            return grouped

        def regroup_on_gpsimd(raw, grouped):
            nc.gpsimd.tensor_scalar(
                out=grouped, in0=raw.rearrange("p t n -> p n t"), scalar1=1.0, scalar2=0.0, op0=MULT, op1=ADD
            )

        def quantise_weight(grouped, codes, scales, half):
            cols = slice(half * BANK, (half + 1) * BANK)
            nc.vector.quantize_mx(
                out=codes[:, cols].bitcast(FP8X4),
                scales=scales[:, cols],
                in_=grouped[:, cols, :].rearrange("p n t -> p (n t)"),
            )

        def transpose_tile(rows):
            words = rows.bitcast(F32)
            turned = psum_t.tile([P, PASSES * 2, B], F32, tag="turned")
            for q in range(PASSES * 2):
                nc.tensor.transpose(turned[:, q, :], words[:, q * P : (q + 1) * P], ident_f32[:])
            return turned

        def regroup_tile(turned, grouped_words):
            nc.scalar.copy(out=grouped_words, in_=turned[:].rearrange("p (c u) b -> p c b u", u=2))

        def prepare_x_pair(j):
            grouped = x_stage.tile([P, PAIR * D], BF16, tag="x_grouped", align_bytes=64)
            words = grouped[:].bitcast(F32).rearrange("p (c i b u) -> p c i b u", c=PASSES, i=PAIR, u=2)
            turned = [transpose_tile(x_raw[j][:, i, :]) for i in range(PAIR)]
            for i in range(PAIR):
                regroup_tile(turned[i], words[:, :, i])
            return grouped

        def quantise_x_pair(grouped):
            codes = x_mx.tile([P, PASSES, PAIR * B], U32, tag="x_codes", align_bytes=64)
            scales = x_mx.tile([P, PASSES, PAIR * B], U8, tag="x_scales", align_bytes=64)
            nc.vector.quantize_mx(
                out=codes[:].rearrange("p c n -> p (c n)").bitcast(FP8X4),
                scales=scales[:].rearrange("p c n -> p (c n)"),
                in_=grouped[:],
            )
            return codes, scales

        def first_layer_bank(first_pass, half, outputs, codes, scales):
            width = BANK // len(outputs)
            bank = psum_mm.tile([P, len(outputs), width], F32, tag="bank")
            for k, t in enumerate(outputs):
                cols = slice(half * BANK + t * P, half * BANK + (t + 1) * P)
                for c in range(PASSES):
                    nc.tensor.matmul_mx(
                        out=bank[:, k, :],
                        lhsT=w1_codes[:, first_pass + c, cols].bitcast(FP8X4),
                        lhsT_scale=w1_scales[:, first_pass + c, cols],
                        rhs=codes[:, c, :].bitcast(FP8X4),
                        rhs_scale=scales[:, c, :],
                        start=(c == 0),
                        stop=(c == PASSES - 1),
                    )
            return bank

        know = keep.tile([P, HALVES, 2, B, 2], F32)

        def first_layer_half(half, codes, scales, g_grouped):
            pre = g_stage.tile([P, 2, PAIR * B, 2], F32, tag="pre")
            for v in range(2):
                bank = first_layer_bank(0, half, (2 * v, 2 * v + 1), codes, scales)
                nc.vector.tensor_tensor(
                    out=pre[:, v].rearrange("p (i b) e -> p i b e", i=PAIR),
                    in0=bank[:].rearrange("p e (i b) -> p i b e", i=PAIR),
                    in1=know[:, half, v].unsqueeze(1).to_broadcast([P, PAIR, B, 2]),
                    op=ADD,
                )
            nc.scalar.activation(
                out=g_grouped[:, half * D : (half + 1) * D].rearrange("p (n v e) -> p n v e", v=2, e=2),
                in_=pre[:].rearrange("p v n e -> p n v e"),
                func=GELU,
            )

        def quantise_g_pair(j, g_grouped):
            nc.vector.quantize_mx(
                out=g_codes[:, j].rearrange("p c i b -> p (c i b)").bitcast(FP8X4),
                scales=g_scales[:, j].rearrange("p c i b -> p (c i b)"),
                in_=g_grouped[:],
            )

        def second_layer_product(bank, j, i, cols):
            for c in range(PASSES):
                nc.tensor.matmul_mx(
                    out=bank[:],
                    lhsT=g_codes[:, j, c, i, :].bitcast(FP8X4),
                    lhsT_scale=g_scales[:, j, c, i, :],
                    rhs=w2_codes[:, c, cols].bitcast(FP8X4),
                    rhs_scale=w2_scales[:, c, cols],
                    start=(c == 0),
                    stop=(c == PASSES - 1),
                )

        def finish(z, j, i, cols):
            nc.scalar.activation(out=z, in_=z, func=TANH)
            nc.sync.dma_start(out=out[:, j * PAIR + i, cols], in_=z)

        def half_columns(half):
            return slice(half * BANK, (half + 1) * BANK)

        def second_layer_half(j, half, tiles):
            for i in tiles:
                pieces = [half_columns(half)]
                if j == GROUPS - 1 and half == HALVES - 1 and i == PAIR - 1:
                    pieces = [slice(D - BANK, D - BANK // 2), slice(D - BANK // 2, D)]
                z = o_stage.tile([P, BANK], F32, tag="z", name="z")
                for cols in pieces:
                    bank = psum_mm.tile([P, cols.stop - cols.start], F32, tag="bank", name="bank")
                    second_layer_product(bank, j, i, cols)
                    part = z[:, cols.start - half * BANK : cols.stop - half * BANK]
                    nc.vector.tensor_tensor(out=part, in0=bank[:], in1=b2_all[:, cols], op=ADD)
                    finish(part, j, i, cols)

        def add_on_gpsimd(j, half, i):
            cols = half_columns(half)
            bank = psum_t.tile([P, BANK], F32, tag="turned", name="bank_aside")
            second_layer_product(bank, j, i, cols)
            z = o_stage.tile([P, BANK], F32, tag="z", name="z")
            nc.scalar.copy(out=z[:], in_=bank[:])
            nc.gpsimd.tensor_tensor(out=z[:], in0=z[:], in1=b2_all[:, cols], op=ADD)
            return z

        def quantise_w1(grouped, c, half):
            quantise_weight(grouped, w1_codes[:, c, :], w1_scales[:, c, :], half)

        def add_knowledge(half):
            nc.vector.tensor_tensor(
                out=know[:, half],
                in0=know_banks[half][:].rearrange("p (v e) b -> p v b e", v=2),
                in1=b1_cols[:, half * PACK : (half + 1) * PACK]
                .rearrange("p (v e) -> p v e", v=2)
                .unsqueeze(2)
                .to_broadcast([P, 2, B, 2]),
                op=ADD,
            )

        grouped_2 = w_stage.tile([P, D, PACK], BF16, tag="w_grouped", name="grouped_2", align_bytes=64)
        regroup_columns(nc.vector.tensor_copy, w1_halves[2, 0][:], grouped_2[:, 0:BANK, :])
        wk_turned = transpose_tile(wk_raw[:])
        wk_grouped = keep.tile([P, D], BF16, align_bytes=64)
        regroup_tile(wk_turned, wk_grouped[:].bitcast(F32).rearrange("p (c b u) -> p c b u", c=PASSES, u=2))
        b1_turned = psum_t.tile([P, P], BF16, tag="turned")
        nc.tensor.transpose(b1_turned[:], b1_rows[:], ident_bf16[:])
        quantise_w1(grouped_2, 2, 0)
        more = EARLY_COLS - BANK
        regroup_columns(nc.vector.tensor_copy, w1_halves[2, 1][:, :, 0:more], grouped_2[:, BANK:EARLY_COLS, :])
        regroup_columns(nc.scalar.copy, w1_halves[2, 1][:, :, more:BANK], grouped_2[:, EARLY_COLS:D, :])
        nc.vector.quantize_mx(
            out=wk_codes[:].rearrange("p c b -> p (c b)").bitcast(FP8X4),
            scales=wk_scales[:].rearrange("p c b -> p (c b)"),
            in_=wk_grouped[:],
        )
        b1_cols = keep.tile([P, D // P], F32)
        nc.vector.tensor_copy(out=b1_cols[:], in_=b1_turned[:, 0 : D // P])
        quantise_w1(grouped_2, 2, 1)
        grouped_3 = regroup_weight(w1_raw[3], VECTOR_COLS[3])
        quantise_w1(grouped_3, 3, 0)
        x_grouped = {0: prepare_x_pair(0)}
        quantise_w1(grouped_3, 3, 1)
        know_banks = [first_layer_bank(PASSES, half, range(PACK), wk_codes, wk_scales) for half in range(HALVES)]
        grouped_0 = regroup_weight(w1_raw[0], VECTOR_COLS[0])
        x_quant = {0: quantise_x_pair(x_grouped[0])}
        quantise_w1(grouped_0, 0, 0)
        add_knowledge(0)
        grouped_1 = regroup_weight(w1_raw[1], VECTOR_COLS[1])
        quantise_w1(grouped_0, 0, 1)
        quantise_w1(grouped_1, 1, 0)
        add_knowledge(1)
        quantise_w1(grouped_1, 1, 1)
        x_grouped[1] = prepare_x_pair(1)

        w2_grouped = {
            (c, half): w2_stage.tile([P, BANK, PACK], BF16, tag="w2_grouped", name="w2_grouped", align_bytes=64)
            for half in range(HALVES)
            for c in range(PASSES)
        }
        pieces = [(c, half, k) for half in range(HALVES) for c in range(PASSES) for k in range(2 + 2 * half)]
        gate = keep.tile([P, len(pieces)], U32)

        def run_aside(count, behind):
            left = len(pieces)
            nc.gpsimd.tensor_copy(out=gate[:, left - 1 : left], in_=behind)
            for turn in range(count):
                piece = pieces[0]
                pieces.remove(piece)
                c, half, k = piece
                source = slice(half * BANK + k * P, half * BANK + (k + 1) * P)
                cols = slice(k * P, (k + 1) * P)
                regroup_on_gpsimd(w2_raw[c][:, :, source], w2_grouped[c, half][:, cols, :])

        def regroup_w2_on_scalar(c):
            cols = slice(2 * P, BANK)
            regroup_columns(nc.scalar.copy, w2_raw[c][:, :, cols], w2_grouped[c, 0][:, cols, :])

        def quantise_w2(c, half):
            cols = slice(half * BANK, (half + 1) * BANK)
            nc.vector.quantize_mx(
                out=w2_codes[:, c, cols].bitcast(FP8X4),
                scales=w2_scales[:, c, cols],
                in_=w2_grouped[c, half][:].rearrange("p n t -> p (n t)"),
            )

        g_grouped = {}
        for j in range(GROUPS + LAG):
            if j == 0:
                run_aside(2, w1_codes[:, 1, D - 1 : D])
                regroup_w2_on_scalar(0)
            if j < GROUPS:
                g_grouped[j] = g_stage.tile([P, PAIR * D], BF16, tag="g_grouped", name="g_grouped", align_bytes=64)
                for half in range(HALVES):
                    first_layer_half(half, x_quant[j][0], x_quant[j][1], g_grouped[j])
            if j + 1 < GROUPS:
                x_quant[j + 1] = quantise_x_pair(x_grouped[j + 1])
            if j + 2 < GROUPS:
                x_grouped[j + 2] = prepare_x_pair(j + 2)
            if j == 0:
                regroup_w2_on_scalar(1)
            if 1 <= j <= GROUPS:
                quantise_g_pair(j - 1, g_grouped[j - 1])
            if j < PASSES:
                quantise_w2(j, 0)
                run_aside(2, w2_codes[:, j, BANK - 1 : BANK])
            elif j < SECOND_HALF_READY:
                run_aside(3, g_codes[:, j - 1, 0, 0, 0:1])
            if j == SECOND_HALF_READY:
                for c in range(PASSES):
                    quantise_w2(c, 1)
            late = 2 * (j - SECOND_HALF_READY - 1)
            catch_up = [p for p in (late, late + 1) if p >= 0] if j < GROUPS else [j - LAG]
            over_gpsimd = catch_up if j == GROUPS - 2 else []
            aside = [add_on_gpsimd(p, 1, 0) for p in over_gpsimd]
            if j >= LAG:
                second_layer_half(j - LAG, 0, range(PAIR))
            for p in catch_up:
                second_layer_half(p, 1, range(1 if over_gpsimd else 0, PAIR))
            for z, p in zip(aside, over_gpsimd):
                finish(z[:], p, 0, half_columns(1))
